import numpy as np
import ml_dtypes


def mxq(x, axis, fmt="e4m3"):
    dtype, down = {"e4m3": (ml_dtypes.float8_e4m3fn, 7), "e5m2": (ml_dtypes.float8_e5m2, 14)}[fmt]
    v = np.moveaxis(np.asarray(x, np.float32).astype(ml_dtypes.bfloat16).astype(np.float64), axis, -1)
    blocks = v.reshape(v.shape[:-1] + (-1, 32))
    amax = np.abs(blocks).max(-1, keepdims=True)
    byte = np.maximum(np.where(amax > 0, np.frexp(amax)[1] - 1 + 127, 0) - down, 1)
    scale = np.exp2(byte - 127.0)
    codes = (blocks / scale).astype(np.float32).astype(dtype).astype(np.float64)
    return np.moveaxis((codes * scale).reshape(v.shape), -1, axis)


WIDE = False


def mx_kscale(k):
    if not WIDE:
        return np.ones(k)
    levels = np.array([10, -10, 5, -5, 0])
    a = np.random.permutation(np.resize(levels, k // 512 * 4)).reshape(k // 512, 4)
    idx = np.arange(k)
    return np.exp2(a[idx // 512, idx % 128 // 32])


BF16 = ml_dtypes.bfloat16


def bf(x):
    return np.asarray(x, np.float32).astype(BF16)


def f64(x):
    return np.asarray(x).astype(np.float64)


E2M1 = np.array([0.0, 0.5, 1.0, 1.5, 2.0, 3.0, 4.0, 6.0, -0.0, -0.5, -1.0, -1.5, -2.0, -3.0, -4.0, -6.0])


def pack_weight(w, fmt):
    k, n = w.shape
    w = f64(bf(w)).reshape(k // 32, 32, n)
    amax = np.abs(w).max(1)
    if fmt == "e4m3":
        byte = np.frexp(amax)[1] - 1 + 127 - 7
    else:
        mant, ex = np.frexp(amax / 6.0)
        byte = np.where(mant > 0.5, ex, ex - 1) + 127
    byte = np.clip(np.where(amax > 0, byte, 1), 1, 254)
    scaled = (w * np.exp2(127.0 - byte)[:, None, :]).reshape(k, n).astype(np.float32)
    by_word = np.ascontiguousarray(scaled.reshape(k // 512, 128, 4, n).transpose(0, 1, 3, 2))
    if fmt == "e4m3":
        words = by_word.astype(ml_dtypes.float8_e4m3fn).view(np.uint8)
    else:
        c = by_word.astype(ml_dtypes.float4_e2m1fn).view(np.uint8) & 0xF
        words = c[..., 0::2] | (c[..., 1::2] << 4)
    return np.ascontiguousarray(words), np.ascontiguousarray(byte.astype(np.uint8).reshape(k // 512, 16, n))


def unpack_weight(words, scales, fmt):
    g, p, n, _ = words.shape
    if fmt == "e4m3":
        vals = np.ascontiguousarray(words).view(ml_dtypes.float8_e4m3fn).astype(np.float64)
    else:
        nib = np.empty((g, p, n, 4), np.uint8)
        nib[..., 0::2] = words & 0xF
        nib[..., 1::2] = words >> 4
        vals = E2M1[nib]
    vals = vals * np.repeat(np.exp2(scales.astype(np.float64) - 127.0), 8, axis=1)[..., None]
    return vals.transpose(0, 1, 3, 2).reshape(g * 512, n)


B, T, V, C, K, R = 2, 8, 32, 8192, 512, 256
FMT = "e4m3"


def setup_inputs():
    n = np.random.standard_normal
    s = mx_kscale(C)
    x = 0.7 * n((B, 1, V, C)) + 0.7 * n((B, T, V, C))
    A = bf(np.eye(V) + 0.1 * n((K, V, V)))
    lam = bf(0.25 + 0.1 * np.random.random(1))
    phi_w_words, phi_w_scales = pack_weight(n((C, K)) / np.sqrt(C) / s[:, None], FMT)
    phi_b = bf(0.3 * n(K))
    theta_w_words, theta_w_scales = pack_weight(n((C, K)) / np.sqrt(C) / s[:, None], FMT)
    theta_b = bf(0.3 * n(K))
    kappa_w_words, kappa_w_scales = pack_weight(n((K, K)) / np.sqrt(K), FMT)
    kappa_b = bf(0.3 * n(K))
    return {
        "x": bf(x * s),
        "A": A,
        "lam": lam,
        "phi_w_words": phi_w_words,
        "phi_w_scales": phi_w_scales,
        "phi_b": phi_b,
        "theta_w_words": theta_w_words,
        "theta_w_scales": theta_w_scales,
        "theta_b": theta_b,
        "kappa_w_words": kappa_w_words,
        "kappa_w_scales": kappa_w_scales,
        "kappa_b": kappa_b,
    }


def reference(x, A, lam, phi_w_words, phi_w_scales, phi_b, theta_w_words, theta_w_scales, theta_b, kappa_w_words, kappa_w_scales, kappa_b):
    xq = mxq(f64(x), 3, "e4m3")
    phi_x = ((xq @ unpack_weight(phi_w_words, phi_w_scales, FMT)) + f64(phi_b)).mean(axis=1)
    theta_x = ((xq @ unpack_weight(theta_w_words, theta_w_scales, FMT)) + f64(theta_b)).mean(axis=1)
    F_ij = np.tanh(phi_x[:, :, None, :] - theta_x[:, None, :, :])
    A_hat = np.transpose((mxq(F_ij, 3, "e4m3") @ unpack_weight(kappa_w_words, kappa_w_scales, FMT)) + f64(kappa_b), (0, 3, 1, 2))
    return f64(A)[None] + f64(lam) * A_hat

@@ -1,0 +1,299 @@
+from contextlib import ExitStack
+
+import concourse.masks as masks
+import concourse.mybir as mybir
+
+F32 = mybir.dt.float32
+BF16 = mybir.dt.bfloat16
+I32 = mybir.dt.int32
+U32 = mybir.dt.uint32
+U8 = mybir.dt.uint8
+FP8X4 = mybir.dt.float8_e4m3fn_x4
+ALU = mybir.AluOpType
+ACT = mybir.ActivationFunctionType
+AXIS = mybir.AxisListType
+
+P = 128
+PACK = 4
+GROUP = P * PACK
+QUADRANTS = 4
+PLANES_PER_TILE = 4
+
+BATCHES, TIMES, JOINTS, FEATURES, CHANNELS = 2, 8, 32, 8192, 512
+ROW_TILES = TIMES * JOINTS // P
+N_GROUPS = FEATURES // GROUP
+WORDS = GROUP // 2
+
+GROUPS_PER_ROUND = 2
+ROUNDS_PER_BATCH = N_GROUPS // GROUPS_PER_ROUND
+N_ROUNDS = BATCHES * ROUNDS_PER_BATCH
+ROUND_COLS = GROUPS_PER_ROUND * GROUP
+X_AHEAD = ROUNDS_PER_BATCH + 2
+
+U_CHUNK = 16
+N_CHUNKS = JOINTS // U_CHUNK
+CHUNK_COLS = U_CHUNK * JOINTS
+M_TILES = CHANNELS // P
+
+FLOPS = 2 * BATCHES * TIMES * JOINTS * FEATURES * 2 * CHANNELS + 2 * BATCHES * JOINTS * JOINTS * CHANNELS * CHANNELS
+
+
+def tile_attgcn_pa_k_kernel(
+    tc,
+    x,
+    A,
+    lam,
+    phi_w_words,
+    phi_w_scales,
+    phi_b,
+    theta_w_words,
+    theta_w_scales,
+    theta_b,
+    kappa_w_words,
+    kappa_w_scales,
+    kappa_b,
+    out,
+):
+    nc = tc.nc
+    with ExitStack() as ctx:
+        ctx.enter_context(tc.manual_schedule())
+        keep = ctx.enter_context(tc.tile_pool(name="keep", bufs=1))
+        x_pool = ctx.enter_context(tc.tile_pool(name="x_pool", bufs=X_AHEAD))
+        quant = ctx.enter_context(tc.tile_pool(name="quant", bufs=3))
+        once = ctx.enter_context(tc.tile_pool(name="once", bufs=1))
+        twice = ctx.enter_context(tc.tile_pool(name="twice", bufs=N_CHUNKS))
+        results = ctx.enter_context(tc.tile_pool(name="results", bufs=4))
+        psum_xt = ctx.enter_context(tc.psum_pool(name="psum_xt", bufs=2))
+        psum_acc = ctx.enter_context(tc.psum_pool(name="psum_acc", bufs=1))
+        psum_means = ctx.enter_context(tc.psum_pool(name="psum_means", bufs=1))
+        psum_g = ctx.enter_context(tc.psum_pool(name="psum_g", bufs=3))
+
+        x_rows = [x[b].rearrange("(rt t) v c -> (t v) rt c", rt=ROW_TILES) for b in range(BATCHES)]
+        words_dram = [
+            w.rearrange("g p n t -> p g (n t)").bitcast(I32) for w in (phi_w_words, theta_w_words)
+        ]
+        scales_dram = [phi_w_scales, theta_w_scales]
+        out_rows = [out[b].rearrange("(m p) u v -> p m (u v)", p=P) for b in range(BATCHES)]
+
+        phi_words = keep.tile([P, N_GROUPS, CHANNELS], U32, align_bytes=64)
+        theta_words = keep.tile([P, N_GROUPS, CHANNELS], U32, align_bytes=64)
+        w_words = [phi_words, theta_words]
+        phi_planes = keep.tile([P, N_GROUPS // PLANES_PER_TILE, CHANNELS], U8, align_bytes=64)
+        theta_planes = keep.tile([P, N_GROUPS // PLANES_PER_TILE, CHANNELS], U8, align_bytes=64)
+        w_planes = [phi_planes, theta_planes]
+        kappa_words = keep.tile([P, CHANNELS], U32, align_bytes=64)
+        kappa_plane = keep.tile([P, CHANNELS], U8, align_bytes=64)
+        a_bf = keep.tile([P, M_TILES, JOINTS * JOINTS], BF16)
+        a_plus = keep.tile([P, M_TILES, JOINTS * JOINTS], F32)
+        ident = keep.tile([P, P], F32)
+        time_sum = keep.tile([P, JOINTS], F32)
+        time_mean = keep.tile([P, JOINTS], F32)
+        lam_bf = keep.tile([P, 1], BF16)
+        lam_col = keep.tile([P, 1], F32)
+        kappa_b_bf = keep.tile([P, M_TILES], BF16)
+        lam_kappa_b = keep.tile([P, M_TILES], F32)
+        phi_b_bf = keep.tile([P, PACK], BF16)
+        theta_b_bf = keep.tile([P, PACK], BF16)
+        bias_diff = keep.tile([P, PACK], F32)
+
+        def load_scale_rows(w, s):
+            for quadrant in range(QUADRANTS):
+                nc.sync.dma_start(
+                    out=w_planes[w][32 * quadrant : 32 * quadrant + 16, s, :].bitcast(I32),
+                    in_=scales_dram[w][
+                        PLANES_PER_TILE * s : PLANES_PER_TILE * (s + 1), 4 * quadrant : 4 * quadrant + 4, :
+                    ].bitcast(I32),
+                )
+
+        def load_words(w, r):
+            groups = slice(GROUPS_PER_ROUND * r, GROUPS_PER_ROUND * (r + 1))
+            nc.sync.dma_start(out=w_words[w][:, groups, :].bitcast(I32), in_=words_dram[w][:, groups, :])
+
+        x_chunks = {}
+
+        def load_x(i):
+            b, r = divmod(i, ROUNDS_PER_BATCH)
+            x_chunk = x_pool.tile([P, ROW_TILES, ROUND_COLS], BF16)
+            nc.sync.dma_start(out=x_chunk[:], in_=x_rows[b][:, :, ROUND_COLS * r : ROUND_COLS * (r + 1)])
+            x_chunks[i] = x_chunk
+
+        for plane in (phi_planes, theta_planes, kappa_plane):
+            nc.vector.memset(plane[:].bitcast(I32), 0)
+
+        rounds_per_plane_tile = PLANES_PER_TILE // GROUPS_PER_ROUND
+        for i in range(X_AHEAD):
+            load_x(i)
+            if i < ROUNDS_PER_BATCH:
+                for w in range(2):
+                    if i % rounds_per_plane_tile == 0:
+                        load_scale_rows(w, i // rounds_per_plane_tile)
+                    load_words(w, i)
+        nc.sync.dma_start(
+            out=kappa_words[:].bitcast(I32), in_=kappa_w_words[0].rearrange("p n t -> p (n t)").bitcast(I32)
+        )
+        for quadrant in range(QUADRANTS):
+            nc.sync.dma_start(
+                out=kappa_plane[32 * quadrant : 32 * quadrant + 4, :].bitcast(I32),
+                in_=kappa_w_scales[0, 4 * quadrant : 4 * quadrant + 4, :].bitcast(I32),
+            )
+        nc.sync.dma_start(out=a_bf[:], in_=A.rearrange("(m p) u v -> p m (u v)", p=P))
+
+        masks.make_identity(nc, ident[:])
+        nc.gpsimd.dma_start(out=lam_bf[:], in_=lam.partition_broadcast(P))
+        nc.gpsimd.dma_start(out=phi_b_bf[:], in_=phi_b.rearrange("(p j) -> p j", j=PACK))
+        nc.gpsimd.dma_start(out=theta_b_bf[:], in_=theta_b.rearrange("(p j) -> p j", j=PACK))
+        with nc.allow_non_contiguous_dma(reason="512 bias values, one output channel to a partition"):
+            nc.gpsimd.dma_start(out=kappa_b_bf[:], in_=kappa_b.rearrange("(m p) -> p m", p=P))
+        nc.gpsimd.tensor_copy(out=lam_col[:], in_=lam_bf[:])
+        nc.gpsimd.tensor_tensor(out=bias_diff[:], in0=theta_b_bf[:], in1=phi_b_bf[:], op=ALU.subtract)
+        nc.gpsimd.tensor_scalar(
+            out=lam_kappa_b[:], in0=kappa_b_bf[:], scalar1=lam_col[:, 0:1], scalar2=0.0, op0=ALU.mult, op1=ALU.add
+        )
+        for m in range(M_TILES):
+            nc.gpsimd.tensor_scalar(
+                out=a_plus[:, m, :],
+                in0=a_bf[:, m, :],
+                scalar1=1.0,
+                scalar2=lam_kappa_b[:, m : m + 1],
+                op0=ALU.mult,
+                op1=ALU.add,
+            )
+        nc.vector.tensor_reduce(
+            out=time_sum[:], in_=ident[:].rearrange("q (t u) -> q u t", u=JOINTS), axis=AXIS.X, op=ALU.add
+        )
+        nc.vector.tensor_scalar(out=time_mean[:], in0=time_sum[:], scalar1=1.0 / TIMES, scalar2=None, op0=ALU.mult)
+
+        x_quantised = {}
+
+        def transpose_round(i):
+            x_chunk = x_chunks[i]
+            grouped = quant.tile([P, GROUPS_PER_ROUND, ROW_TILES * P * PACK], BF16, align_bytes=64)
+            for gi in range(GROUPS_PER_ROUND):
+                xt = psum_xt.tile([P, ROW_TILES, 2, P], F32)
+                for rt in range(ROW_TILES):
+                    x_words = x_chunk[:, rt, :].bitcast(F32)
+                    for half in range(2):
+                        nc.tensor.transpose(
+                            xt[:, rt, half, :], x_words[:, WORDS * gi + half : WORDS * (gi + 1) : 2], ident[:]
+                        )
+                nc.scalar.copy(
+                    out=grouped[:, gi, :].bitcast(F32).rearrange("p (rt q h) -> p rt q h", rt=ROW_TILES, h=2),
+                    in_=xt[:].rearrange("p rt h q -> p rt q h"),
+                )
+            x_codes = quant.tile([P, GROUPS_PER_ROUND * ROW_TILES * P], U32, align_bytes=64)
+            x_scales = quant.tile([P, GROUPS_PER_ROUND * ROW_TILES * P], U8, align_bytes=64)
+            nc.vector.quantize_mx(
+                out=x_codes[:].bitcast(FP8X4), scales=x_scales[:], in_=grouped[:].rearrange("p g c -> p (g c)")
+            )
+            x_quantised[i] = (x_codes, x_scales)
+
+        sums = {}
+
+        def multiply_round(i):
+            b, r = divmod(i, ROUNDS_PER_BATCH)
+            if r == 0:
+                acc_phi = psum_acc.tile([P, CHANNELS], F32)
+                acc_theta = psum_acc.tile([P, CHANNELS], F32)
+                sums[b] = [acc_phi, acc_theta]
+            x_codes, x_scales = x_quantised[i]
+            for gi in range(GROUPS_PER_ROUND):
+                g = GROUPS_PER_ROUND * r + gi
+                s, plane_start = g // PLANES_PER_TILE, 4 * (g % PLANES_PER_TILE)
+                for rt in range(ROW_TILES):
+                    rows = slice((gi * ROW_TILES + rt) * P, (gi * ROW_TILES + rt + 1) * P)
+                    for w in range(2):
+                        nc.tensor.matmul_mx(
+                            out=sums[b][w][:],
+                            lhsT=x_codes[:, rows].bitcast(FP8X4),
+                            lhsT_scale=x_scales[:, rows],
+                            rhs=w_words[w][:, g, :].bitcast(FP8X4),
+                            rhs_scale=w_planes[w][plane_start:P, s, :],
+                            start=(g == 0 and rt == 0),
+                            stop=(g == N_GROUPS - 1 and rt == ROW_TILES - 1),
+                        )
+
+        held = {}
+
+        def sums_leave_psum(b):
+            y_phi = once.tile([P, PACK, P], F32)
+            y_theta = once.tile([P, PACK, P], F32)
+            nc.vector.tensor_copy(out=y_phi[:], in_=sums[b][0][:].rearrange("q (p j) -> q j p", j=PACK))
+            nc.scalar.copy(out=y_theta[:], in_=sums[b][1][:].rearrange("q (p j) -> q j p", j=PACK))
+            held["y"] = [y_phi, y_theta]
+
+        def joint_means(b):
+            means = psum_means.tile([P, 2, PACK, JOINTS], F32)
+            for w in range(2):
+                for j in range(PACK):
+                    nc.tensor.matmul(
+                        means[:, w, j, :], lhsT=held["y"][w][:, j, :], rhs=time_mean[:], start=True, stop=True
+                    )
+            th = once.tile([P, JOINTS, PACK], F32)
+            nc.vector.tensor_tensor(
+                out=th[:],
+                in0=means[:, 1].rearrange("p j v -> p v j"),
+                in1=bias_diff[:].unsqueeze(1).to_broadcast([P, JOINTS, PACK]),
+                op=ALU.add,
+            )
+            held["means"], held["th"] = means, th
+
+        def tanh_of_differences(b, c):
+            shape = [P, U_CHUNK, JOINTS, PACK]
+            d = twice.tile(shape, F32)
+            nc.vector.tensor_tensor(
+                out=d[:],
+                in0=held["means"][:, 0, :, U_CHUNK * c : U_CHUNK * (c + 1)]
+                .rearrange("p j u -> p u j")
+                .unsqueeze(2)
+                .to_broadcast(shape),
+                in1=held["th"][:].unsqueeze(1).to_broadcast(shape),
+                op=ALU.subtract,
+            )
+            f = twice.tile([P, CHUNK_COLS * PACK], BF16, align_bytes=64)
+            nc.scalar.activation(out=f[:], in_=d[:].rearrange("p u v j -> p (u v j)"), func=ACT.Tanh)
+            held["f", c] = f
+
+        def outputs(b, c):
+            f_codes = twice.tile([P, CHUNK_COLS], U32, align_bytes=64)
+            f_scales = twice.tile([P, CHUNK_COLS], U8, align_bytes=64)
+            nc.vector.quantize_mx(out=f_codes[:].bitcast(FP8X4), scales=f_scales[:], in_=held["f", c][:])
+            cols = slice(CHUNK_COLS * c, CHUNK_COLS * (c + 1))
+            for m in range(M_TILES):
+                channels = slice(P * m, P * (m + 1))
+                g_ps = psum_g.tile([P, CHUNK_COLS], F32)
+                nc.tensor.matmul_mx(
+                    out=g_ps[:],
+                    lhsT=kappa_words[:, channels].bitcast(FP8X4),
+                    lhsT_scale=kappa_plane[:, channels],
+                    rhs=f_codes[:].bitcast(FP8X4),
+                    rhs_scale=f_scales[:],
+                    start=True,
+                    stop=True,
+                )
+                result = results.tile([P, CHUNK_COLS], F32)
+                nc.vector.scalar_tensor_tensor(
+                    out=result[:],
+                    in0=g_ps[:],
+                    scalar=lam_col[:, 0:1],
+                    in1=a_plus[:, m, cols],
+                    op0=ALU.mult,
+                    op1=ALU.add,
+                )
+                nc.sync.dma_start(out=out_rows[b][:, m, cols], in_=result[:])
+
+        second_stage = [sums_leave_psum, joint_means]
+        second_stage += [lambda b, c=c: tanh_of_differences(b, c) for c in range(N_CHUNKS)]
+        second_stage += [lambda b, c=c: outputs(b, c) for c in range(N_CHUNKS)]
+
+        transpose_round(0)
+        for i in range(N_ROUNDS):
+            if i + 1 < N_ROUNDS:
+                transpose_round(i + 1)
+            if i + X_AHEAD < N_ROUNDS:
+                load_x(i + X_AHEAD)
+            multiply_round(i)
+            step = i - (ROUNDS_PER_BATCH - 1)
+            if 0 <= step < len(second_stage):
+                second_stage[step](0)
+        for step in second_stage:
+            step(1)

@@ -20,15 +20,16 @@ QUADRANTS = 4
 PLANES_PER_TILE = 4
 
 BATCHES, TIMES, JOINTS, FEATURES, CHANNELS = 2, 8, 32, 8192, 512
-ROW_TILES = TIMES * JOINTS // P
+TILES_PER_BATCH = TIMES * JOINTS // P
+ROW_TILES = BATCHES * TILES_PER_BATCH
+EARLY_TILES = 3
 N_GROUPS = FEATURES // GROUP
-WORDS = GROUP // 2
 
 GROUPS_PER_ROUND = 2
-ROUNDS_PER_BATCH = N_GROUPS // GROUPS_PER_ROUND
-N_ROUNDS = BATCHES * ROUNDS_PER_BATCH
+N_ROUNDS = N_GROUPS // GROUPS_PER_ROUND
 ROUND_COLS = GROUPS_PER_ROUND * GROUP
-X_AHEAD = ROUNDS_PER_BATCH + 2
+ROUND_WORDS = GROUPS_PER_ROUND * P
+X_BUFS = 4
 
 U_CHUNK = 16
 N_CHUNKS = JOINTS // U_CHUNK
@@ -58,17 +59,17 @@ def tile_attgcn_pa_k_kernel(
     with ExitStack() as ctx:
         ctx.enter_context(tc.manual_schedule())
         keep = ctx.enter_context(tc.tile_pool(name="keep", bufs=1))
-        x_pool = ctx.enter_context(tc.tile_pool(name="x_pool", bufs=X_AHEAD))
+        x_pool = ctx.enter_context(tc.tile_pool(name="x_pool", bufs=X_BUFS))
+        regroup = ctx.enter_context(tc.tile_pool(name="regroup", bufs=2))
         quant = ctx.enter_context(tc.tile_pool(name="quant", bufs=3))
         once = ctx.enter_context(tc.tile_pool(name="once", bufs=1))
         twice = ctx.enter_context(tc.tile_pool(name="twice", bufs=N_CHUNKS))
         results = ctx.enter_context(tc.tile_pool(name="results", bufs=4))
-        psum_xt = ctx.enter_context(tc.psum_pool(name="psum_xt", bufs=2))
-        psum_acc = ctx.enter_context(tc.psum_pool(name="psum_acc", bufs=1))
+        psum_acc = ctx.enter_context(tc.psum_pool(name="psum_acc", bufs=BATCHES))
         psum_means = ctx.enter_context(tc.psum_pool(name="psum_means", bufs=1))
-        psum_g = ctx.enter_context(tc.psum_pool(name="psum_g", bufs=3))
+        psum_work = ctx.enter_context(tc.psum_pool(name="psum_work", bufs=3))
 
-        x_rows = [x[b].rearrange("(rt t) v c -> (t v) rt c", rt=ROW_TILES) for b in range(BATCHES)]
+        x_rows = x.rearrange("b (rt t) v c -> (t v) (b rt) c", rt=TILES_PER_BATCH)
         words_dram = [
             w.rearrange("g p n t -> p g (n t)").bitcast(I32) for w in (phi_w_words, theta_w_words)
         ]
@@ -81,6 +82,8 @@ def tile_attgcn_pa_k_kernel(
         phi_planes = keep.tile([P, N_GROUPS // PLANES_PER_TILE, CHANNELS], U8, align_bytes=64)
         theta_planes = keep.tile([P, N_GROUPS // PLANES_PER_TILE, CHANNELS], U8, align_bytes=64)
         w_planes = [phi_planes, theta_planes]
+        late_codes = keep.tile([P, ROW_TILES - EARLY_TILES, N_ROUNDS, ROUND_WORDS], U32, align_bytes=64)
+        late_scales = keep.tile([P, ROW_TILES - EARLY_TILES, N_ROUNDS, ROUND_WORDS], U8, align_bytes=64)
         kappa_words = keep.tile([P, CHANNELS], U32, align_bytes=64)
         kappa_plane = keep.tile([P, CHANNELS], U8, align_bytes=64)
         a_bf = keep.tile([P, M_TILES, JOINTS * JOINTS], BF16)
@@ -105,38 +108,30 @@ def tile_attgcn_pa_k_kernel(
                     ].bitcast(I32),
                 )
 
-        def load_words(w, r):
+        rounds_per_plane_tile = PLANES_PER_TILE // GROUPS_PER_ROUND
+
+        def load_weights(r):
             groups = slice(GROUPS_PER_ROUND * r, GROUPS_PER_ROUND * (r + 1))
-            nc.sync.dma_start(out=w_words[w][:, groups, :].bitcast(I32), in_=words_dram[w][:, groups, :])
+            for w in range(2):
+                if r % rounds_per_plane_tile == 0:
+                    load_scale_rows(w, r // rounds_per_plane_tile)
+                nc.sync.dma_start(out=w_words[w][:, groups, :].bitcast(I32), in_=words_dram[w][:, groups, :])
 
         x_chunks = {}
 
-        def load_x(i):
-            b, r = divmod(i, ROUNDS_PER_BATCH)
+        def load_x(r):
             x_chunk = x_pool.tile([P, ROW_TILES, ROUND_COLS], BF16)
-            nc.sync.dma_start(out=x_chunk[:], in_=x_rows[b][:, :, ROUND_COLS * r : ROUND_COLS * (r + 1)])
-            x_chunks[i] = x_chunk
+            nc.sync.dma_start(out=x_chunk[:], in_=x_rows[:, :, ROUND_COLS * r : ROUND_COLS * (r + 1)])
+            x_chunks[r] = x_chunk
 
         for plane in (phi_planes, theta_planes, kappa_plane):
             nc.vector.memset(plane[:].bitcast(I32), 0)
 
-        rounds_per_plane_tile = PLANES_PER_TILE // GROUPS_PER_ROUND
-        for i in range(X_AHEAD):
-            load_x(i)
-            if i < ROUNDS_PER_BATCH:
-                for w in range(2):
-                    if i % rounds_per_plane_tile == 0:
-                        load_scale_rows(w, i // rounds_per_plane_tile)
-                    load_words(w, i)
-        nc.sync.dma_start(
-            out=kappa_words[:].bitcast(I32), in_=kappa_w_words[0].rearrange("p n t -> p (n t)").bitcast(I32)
-        )
-        for quadrant in range(QUADRANTS):
-            nc.sync.dma_start(
-                out=kappa_plane[32 * quadrant : 32 * quadrant + 4, :].bitcast(I32),
-                in_=kappa_w_scales[0, 4 * quadrant : 4 * quadrant + 4, :].bitcast(I32),
-            )
-        nc.sync.dma_start(out=a_bf[:], in_=A.rearrange("(m p) u v -> p m (u v)", p=P))
+        load_x(0)
+        load_x(1)
+        for r in range(X_BUFS - 2):
+            load_weights(r)
+            load_x(r + 2)
 
         masks.make_identity(nc, ident[:])
         nc.gpsimd.dma_start(out=lam_bf[:], in_=lam.partition_broadcast(P))
@@ -149,15 +144,6 @@ def tile_attgcn_pa_k_kernel(
         nc.gpsimd.tensor_scalar(
             out=lam_kappa_b[:], in0=kappa_b_bf[:], scalar1=lam_col[:, 0:1], scalar2=0.0, op0=ALU.mult, op1=ALU.add
         )
-        for m in range(M_TILES):
-            nc.gpsimd.tensor_scalar(
-                out=a_plus[:, m, :],
-                in0=a_bf[:, m, :],
-                scalar1=1.0,
-                scalar2=lam_kappa_b[:, m : m + 1],
-                op0=ALU.mult,
-                op1=ALU.add,
-            )
         nc.vector.tensor_reduce(
             out=time_sum[:], in_=ident[:].rearrange("q (t u) -> q u t", u=JOINTS), axis=AXIS.X, op=ALU.add
         )
@@ -165,51 +151,61 @@ def tile_attgcn_pa_k_kernel(
 
         x_quantised = {}
 
-        def transpose_round(i):
-            x_chunk = x_chunks[i]
-            grouped = quant.tile([P, GROUPS_PER_ROUND, ROW_TILES * P * PACK], BF16, align_bytes=64)
-            for gi in range(GROUPS_PER_ROUND):
-                xt = psum_xt.tile([P, ROW_TILES, 2, P], F32)
-                for rt in range(ROW_TILES):
-                    x_words = x_chunk[:, rt, :].bitcast(F32)
-                    for half in range(2):
-                        nc.tensor.transpose(
-                            xt[:, rt, half, :], x_words[:, WORDS * gi + half : WORDS * (gi + 1) : 2], ident[:]
-                        )
-                nc.scalar.copy(
-                    out=grouped[:, gi, :].bitcast(F32).rearrange("p (rt q h) -> p rt q h", rt=ROW_TILES, h=2),
-                    in_=xt[:].rearrange("p rt h q -> p rt q h"),
-                )
-            x_codes = quant.tile([P, GROUPS_PER_ROUND * ROW_TILES * P], U32, align_bytes=64)
-            x_scales = quant.tile([P, GROUPS_PER_ROUND * ROW_TILES * P], U8, align_bytes=64)
-            nc.vector.quantize_mx(
-                out=x_codes[:].bitcast(FP8X4), scales=x_scales[:], in_=grouped[:].rearrange("p g c -> p (g c)")
+        def prepare(r):
+            x_sorted = regroup.tile([P, ROW_TILES, GROUPS_PER_ROUND, 2, P], F32)
+            nc.vector.tensor_copy(
+                out=x_sorted[:].rearrange("q a g h p -> q (a g) h p"),
+                in_=x_chunks[r][:].bitcast(F32).rearrange("q a (g p h) -> q (a g) h p", g=GROUPS_PER_ROUND, h=2),
             )
-            x_quantised[i] = (x_codes, x_scales)
+            grouped = regroup.tile([P, ROW_TILES, GROUPS_PER_ROUND, P * PACK], BF16, align_bytes=64)
+            for b in range(BATCHES):
+                tiles = slice(TILES_PER_BATCH * b, TILES_PER_BATCH * (b + 1))
+                for gi in range(GROUPS_PER_ROUND):
+                    xt = psum_work.tile([P, TILES_PER_BATCH, 2, P], F32, tag="work")
+                    for rt in range(TILES_PER_BATCH):
+                        for h in range(2):
+                            nc.tensor.transpose(
+                                xt[:, rt, h, :], x_sorted[:, TILES_PER_BATCH * b + rt, gi, h, :], ident[:]
+                            )
+                    nc.scalar.copy(
+                        out=grouped[:, tiles, gi, :].bitcast(F32).rearrange("p rt (q h) -> p rt q h", h=2),
+                        in_=xt[:].rearrange("p rt h q -> p rt q h"),
+                    )
+            x_codes = quant.tile([P, EARLY_TILES, ROUND_WORDS], U32, align_bytes=64)
+            x_scales = quant.tile([P, EARLY_TILES, ROUND_WORDS], U8, align_bytes=64)
+            for a in range(ROW_TILES):
+                if a < EARLY_TILES:
+                    x_quantised[a, r] = (x_codes[:, a, :], x_scales[:, a, :])
+                else:
+                    x_quantised[a, r] = (late_codes[:, a - EARLY_TILES, r, :], late_scales[:, a - EARLY_TILES, r, :])
+                codes, scales = x_quantised[a, r]
+                nc.vector.quantize_mx(
+                    out=codes.bitcast(FP8X4), scales=scales, in_=grouped[:, a].rearrange("p g c -> p (g c)")
+                )
 
-        sums = {}
+        sums = []
+        for b in range(BATCHES):
+            acc_phi = psum_acc.tile([P, CHANNELS], F32)
+            acc_theta = psum_acc.tile([P, CHANNELS], F32)
+            sums.append([acc_phi, acc_theta])
 
-        def multiply_round(i):
-            b, r = divmod(i, ROUNDS_PER_BATCH)
-            if r == 0:
-                acc_phi = psum_acc.tile([P, CHANNELS], F32)
-                acc_theta = psum_acc.tile([P, CHANNELS], F32)
-                sums[b] = [acc_phi, acc_theta]
-            x_codes, x_scales = x_quantised[i]
+        def multiply(r, row_tiles):
             for gi in range(GROUPS_PER_ROUND):
                 g = GROUPS_PER_ROUND * r + gi
                 s, plane_start = g // PLANES_PER_TILE, 4 * (g % PLANES_PER_TILE)
-                for rt in range(ROW_TILES):
-                    rows = slice((gi * ROW_TILES + rt) * P, (gi * ROW_TILES + rt + 1) * P)
+                rows = slice(gi * P, (gi + 1) * P)
+                for a in row_tiles:
+                    b, rt = divmod(a, TILES_PER_BATCH)
+                    codes, scales = x_quantised[a, r]
                     for w in range(2):
                         nc.tensor.matmul_mx(
                             out=sums[b][w][:],
-                            lhsT=x_codes[:, rows].bitcast(FP8X4),
-                            lhsT_scale=x_scales[:, rows],
+                            lhsT=codes[:, rows].bitcast(FP8X4),
+                            lhsT_scale=scales[:, rows],
                             rhs=w_words[w][:, g, :].bitcast(FP8X4),
                             rhs_scale=w_planes[w][plane_start:P, s, :],
                             start=(g == 0 and rt == 0),
-                            stop=(g == N_GROUPS - 1 and rt == ROW_TILES - 1),
+                            stop=(g == N_GROUPS - 1 and rt == TILES_PER_BATCH - 1),
                         )
 
         held = {}
@@ -217,9 +213,9 @@ def tile_attgcn_pa_k_kernel(
         def sums_leave_psum(b):
             y_phi = once.tile([P, PACK, P], F32)
             y_theta = once.tile([P, PACK, P], F32)
-            nc.vector.tensor_copy(out=y_phi[:], in_=sums[b][0][:].rearrange("q (p j) -> q j p", j=PACK))
-            nc.scalar.copy(out=y_theta[:], in_=sums[b][1][:].rearrange("q (p j) -> q j p", j=PACK))
             held["y"] = [y_phi, y_theta]
+            for w in range(2):
+                nc.scalar.copy(out=held["y"][w][:], in_=sums[b][w][:].rearrange("q (p j) -> q j p", j=PACK))
 
         def joint_means(b):
             means = psum_means.tile([P, 2, PACK, JOINTS], F32)
@@ -237,7 +233,7 @@ def tile_attgcn_pa_k_kernel(
             )
             held["means"], held["th"] = means, th
 
-        def tanh_of_differences(b, c):
+        def differences(b, c):
             shape = [P, U_CHUNK, JOINTS, PACK]
             d = twice.tile(shape, F32)
             nc.vector.tensor_tensor(
@@ -249,8 +245,11 @@ def tile_attgcn_pa_k_kernel(
                 in1=held["th"][:].unsqueeze(1).to_broadcast(shape),
                 op=ALU.subtract,
             )
+            held["d", c] = d
+
+        def tanh(b, c):
             f = twice.tile([P, CHUNK_COLS * PACK], BF16, align_bytes=64)
-            nc.scalar.activation(out=f[:], in_=d[:].rearrange("p u v j -> p (u v j)"), func=ACT.Tanh)
+            nc.scalar.activation(out=f[:], in_=held["d", c][:].rearrange("p u v j -> p (u v j)"), func=ACT.Tanh)
             held["f", c] = f
 
         def outputs(b, c):
@@ -260,7 +259,7 @@ def tile_attgcn_pa_k_kernel(
             cols = slice(CHUNK_COLS * c, CHUNK_COLS * (c + 1))
             for m in range(M_TILES):
                 channels = slice(P * m, P * (m + 1))
-                g_ps = psum_g.tile([P, CHUNK_COLS], F32)
+                g_ps = psum_work.tile([P, CHUNK_COLS], F32, tag="work")
                 nc.tensor.matmul_mx(
                     out=g_ps[:],
                     lhsT=kappa_words[:, channels].bitcast(FP8X4),
@@ -281,19 +280,53 @@ def tile_attgcn_pa_k_kernel(
                 )
                 nc.sync.dma_start(out=out_rows[b][:, m, cols], in_=result[:])
 
-        second_stage = [sums_leave_psum, joint_means]
-        second_stage += [lambda b, c=c: tanh_of_differences(b, c) for c in range(N_CHUNKS)]
-        second_stage += [lambda b, c=c: outputs(b, c) for c in range(N_CHUNKS)]
+        def chunk_step(b, s):
+            if s == 0:
+                joint_means(b)
+            if 0 <= s - 1 < N_CHUNKS:
+                tanh(b, s - 1)
+            if s < N_CHUNKS:
+                differences(b, s)
+            if 0 <= s - 2:
+                outputs(b, s - 2)
 
-        transpose_round(0)
-        for i in range(N_ROUNDS):
-            if i + 1 < N_ROUNDS:
-                transpose_round(i + 1)
-            if i + X_AHEAD < N_ROUNDS:
-                load_x(i + X_AHEAD)
-            multiply_round(i)
-            step = i - (ROUNDS_PER_BATCH - 1)
-            if 0 <= step < len(second_stage):
-                second_stage[step](0)
-        for step in second_stage:
-            step(1)
+        n_steps = N_CHUNKS + 2
+
+        prepare(0)
+        for r in range(N_ROUNDS):
+            if r + 1 < N_ROUNDS:
+                prepare(r + 1)
+            if r + X_BUFS - 2 < N_ROUNDS:
+                load_weights(r + X_BUFS - 2)
+            if r + X_BUFS < N_ROUNDS:
+                load_x(r + X_BUFS)
+            multiply(r, range(EARLY_TILES))
+
+        nc.sync.dma_start(
+            out=kappa_words[:].bitcast(I32), in_=kappa_w_words[0].rearrange("p n t -> p (n t)").bitcast(I32)
+        )
+        for quadrant in range(QUADRANTS):
+            nc.sync.dma_start(
+                out=kappa_plane[32 * quadrant : 32 * quadrant + 4, :].bitcast(I32),
+                in_=kappa_w_scales[0, 4 * quadrant : 4 * quadrant + 4, :].bitcast(I32),
+            )
+        nc.sync.dma_start(out=a_bf[:], in_=A.rearrange("(m p) u v -> p m (u v)", p=P))
+        for m in range(M_TILES):
+            nc.gpsimd.tensor_scalar(
+                out=a_plus[:, m, :],
+                in0=a_bf[:, m, :],
+                scalar1=1.0,
+                scalar2=lam_kappa_b[:, m : m + 1],
+                op0=ALU.mult,
+                op1=ALU.add,
+            )
+
+        rounds_per_step = N_ROUNDS // n_steps
+        sums_leave_psum(0)
+        for s in range(n_steps):
+            for r in range(rounds_per_step * s, rounds_per_step * (s + 1)):
+                multiply(r, range(EARLY_TILES, ROW_TILES))
+            chunk_step(0, s)
+        sums_leave_psum(1)
+        for s in range(n_steps):
+            chunk_step(1, s)

@@ -30,6 +30,7 @@ N_ROUNDS = N_GROUPS // GROUPS_PER_ROUND
 ROUND_COLS = GROUPS_PER_ROUND * GROUP
 ROUND_WORDS = GROUPS_PER_ROUND * P
 X_BUFS = 4
+assert 2 * N_GROUPS // PLANES_PER_TILE == N_ROUNDS
 
 U_CHUNK = 16
 N_CHUNKS = JOINTS // U_CHUNK
@@ -99,7 +100,8 @@ def tile_attgcn_pa_k_kernel(
         theta_b_bf = keep.tile([P, PACK], BF16)
         bias_diff = keep.tile([P, PACK], F32)
 
-        def load_scale_rows(w, s):
+        def load_scale_rows(k):
+            w, s = k % 2, k // 2
             for quadrant in range(QUADRANTS):
                 nc.sync.dma_start(
                     out=w_planes[w][32 * quadrant : 32 * quadrant + 16, s, :].bitcast(I32),
@@ -108,21 +110,22 @@ def tile_attgcn_pa_k_kernel(
                     ].bitcast(I32),
                 )
 
-        rounds_per_plane_tile = PLANES_PER_TILE // GROUPS_PER_ROUND
-
-        def load_weights(r):
+        def load_words(r):
             groups = slice(GROUPS_PER_ROUND * r, GROUPS_PER_ROUND * (r + 1))
             for w in range(2):
-                if r % rounds_per_plane_tile == 0:
-                    load_scale_rows(w, r // rounds_per_plane_tile)
                 nc.sync.dma_start(out=w_words[w][:, groups, :].bitcast(I32), in_=words_dram[w][:, groups, :])
 
         x_chunks = {}
 
         def load_x(r):
             x_chunk = x_pool.tile([P, ROW_TILES, ROUND_COLS], BF16)
-            nc.sync.dma_start(out=x_chunk[:], in_=x_rows[:, :, ROUND_COLS * r : ROUND_COLS * (r + 1)])
+            for b in range(BATCHES):
+                tiles = slice(TILES_PER_BATCH * b, TILES_PER_BATCH * (b + 1))
+                nc.sync.dma_start(
+                    out=x_chunk[:, tiles, :], in_=x_rows[:, tiles, ROUND_COLS * r : ROUND_COLS * (r + 1)]
+                )
             x_chunks[r] = x_chunk
+            load_scale_rows(r)
 
         for plane in (phi_planes, theta_planes, kappa_plane):
             nc.vector.memset(plane[:].bitcast(I32), 0)
@@ -130,7 +133,7 @@ def tile_attgcn_pa_k_kernel(
         load_x(0)
         load_x(1)
         for r in range(X_BUFS - 2):
-            load_weights(r)
+            load_words(r)
             load_x(r + 2)
 
         masks.make_identity(nc, ident[:])
@@ -151,12 +154,22 @@ def tile_attgcn_pa_k_kernel(
 
         x_quantised = {}
 
-        def prepare(r):
+        x_sorted_of = {}
+
+        def sort_words(r):
             x_sorted = regroup.tile([P, ROW_TILES, GROUPS_PER_ROUND, 2, P], F32)
-            nc.vector.tensor_copy(
-                out=x_sorted[:].rearrange("q a g h p -> q (a g) h p"),
-                in_=x_chunks[r][:].bitcast(F32).rearrange("q a (g p h) -> q (a g) h p", g=GROUPS_PER_ROUND, h=2),
-            )
+            for b in range(BATCHES):
+                tiles = slice(TILES_PER_BATCH * b, TILES_PER_BATCH * (b + 1))
+                nc.vector.tensor_copy(
+                    out=x_sorted[:, tiles].rearrange("q a g h p -> q (a g) h p"),
+                    in_=x_chunks[r][:, tiles, :]
+                    .bitcast(F32)
+                    .rearrange("q a (g p h) -> q (a g) h p", g=GROUPS_PER_ROUND, h=2),
+                )
+            x_sorted_of[r] = x_sorted
+
+        def transpose_and_quantise(r):
+            x_sorted = x_sorted_of[r]
             grouped = regroup.tile([P, ROW_TILES, GROUPS_PER_ROUND, P * PACK], BF16, align_bytes=64)
             for b in range(BATCHES):
                 tiles = slice(TILES_PER_BATCH * b, TILES_PER_BATCH * (b + 1))
@@ -281,8 +294,6 @@ def tile_attgcn_pa_k_kernel(
                 nc.sync.dma_start(out=out_rows[b][:, m, cols], in_=result[:])
 
         def chunk_step(b, s):
-            if s == 0:
-                joint_means(b)
             if 0 <= s - 1 < N_CHUNKS:
                 tanh(b, s - 1)
             if s < N_CHUNKS:
@@ -292,12 +303,16 @@ def tile_attgcn_pa_k_kernel(
 
         n_steps = N_CHUNKS + 2
 
-        prepare(0)
+        sort_words(0)
+        sort_words(1)
+        transpose_and_quantise(0)
         for r in range(N_ROUNDS):
+            if r + 2 < N_ROUNDS:
+                sort_words(r + 2)
             if r + 1 < N_ROUNDS:
-                prepare(r + 1)
+                transpose_and_quantise(r + 1)
             if r + X_BUFS - 2 < N_ROUNDS:
-                load_weights(r + X_BUFS - 2)
+                load_words(r + X_BUFS - 2)
             if r + X_BUFS < N_ROUNDS:
                 load_x(r + X_BUFS)
             multiply(r, range(EARLY_TILES))
@@ -323,10 +338,13 @@ def tile_attgcn_pa_k_kernel(
 
         rounds_per_step = N_ROUNDS // n_steps
         sums_leave_psum(0)
+        joint_means(0)
         for s in range(n_steps):
             for r in range(rounds_per_step * s, rounds_per_step * (s + 1)):
                 multiply(r, range(EARLY_TILES, ROW_TILES))
+            if s == n_steps - 1:
+                sums_leave_psum(1)
             chunk_step(0, s)
-        sums_leave_psum(1)
+        joint_means(1)
         for s in range(n_steps):
             chunk_step(1, s)

@@ -20,22 +20,24 @@ QUADRANTS = 4
 PLANES_PER_TILE = 4
 
 BATCHES, TIMES, JOINTS, FEATURES, CHANNELS = 2, 8, 32, 8192, 512
-TILES_PER_BATCH = TIMES * JOINTS // P
-ROW_TILES = BATCHES * TILES_PER_BATCH
-EARLY_TILES = 3
+T_HALF = TIMES // 2
+HALF = JOINTS // 2
+ROW_TILES = 2 * BATCHES
 N_GROUPS = FEATURES // GROUP
+PHI, THETA = 0, 1
 
-GROUPS_PER_ROUND = 2
-N_ROUNDS = N_GROUPS // GROUPS_PER_ROUND
-ROUND_COLS = GROUPS_PER_ROUND * GROUP
-ROUND_WORDS = GROUPS_PER_ROUND * P
-X_BUFS = 4
-assert 2 * N_GROUPS // PLANES_PER_TILE == N_ROUNDS
+ROUND_GROUPS = 2
+N_ROUNDS = N_GROUPS // ROUND_GROUPS
+ROUND_COLS = ROUND_GROUPS * GROUP
+BLOCKS = ROW_TILES * ROUND_GROUPS
+X_BUFS = 3
+LAG = 0
 
-U_CHUNK = 16
+U_CHUNK = 8
 N_CHUNKS = JOINTS // U_CHUNK
 CHUNK_COLS = U_CHUNK * JOINTS
 M_TILES = CHANNELS // P
+BY_SCALAR = ()
 
 FLOPS = 2 * BATCHES * TIMES * JOINTS * FEATURES * 2 * CHANNELS + 2 * BATCHES * JOINTS * JOINTS * CHANNELS * CHANNELS
 
@@ -62,18 +64,15 @@ def tile_attgcn_pa_k_kernel(
         keep = ctx.enter_context(tc.tile_pool(name="keep", bufs=1))
         x_pool = ctx.enter_context(tc.tile_pool(name="x_pool", bufs=X_BUFS))
         regroup = ctx.enter_context(tc.tile_pool(name="regroup", bufs=2))
-        quant = ctx.enter_context(tc.tile_pool(name="quant", bufs=3))
-        once = ctx.enter_context(tc.tile_pool(name="once", bufs=1))
-        twice = ctx.enter_context(tc.tile_pool(name="twice", bufs=N_CHUNKS))
-        results = ctx.enter_context(tc.tile_pool(name="results", bufs=4))
-        psum_acc = ctx.enter_context(tc.psum_pool(name="psum_acc", bufs=BATCHES))
-        psum_means = ctx.enter_context(tc.psum_pool(name="psum_means", bufs=1))
-        psum_work = ctx.enter_context(tc.psum_pool(name="psum_work", bufs=3))
+        quant = ctx.enter_context(tc.tile_pool(name="quant", bufs=LAG + 2))
+        twice = ctx.enter_context(tc.tile_pool(name="twice", bufs=2))
+        results = ctx.enter_context(tc.tile_pool(name="results", bufs=6))
+        psum_acc = ctx.enter_context(tc.psum_pool(name="psum_acc", bufs=4))
+        psum_work = ctx.enter_context(tc.psum_pool(name="psum_work", bufs=4))
 
-        x_rows = x.rearrange("b (rt t) v c -> (t v) (b rt) c", rt=TILES_PER_BATCH)
-        words_dram = [
-            w.rearrange("g p n t -> p g (n t)").bitcast(I32) for w in (phi_w_words, theta_w_words)
-        ]
+        x_by_time = x.rearrange("b (rt t) v c -> (t v) (b rt) c", t=T_HALF)
+        x_by_joint = x.rearrange("b t v c -> b v t c")
+        words_dram = [w.rearrange("g p n t -> p g (n t)").bitcast(I32) for w in (phi_w_words, theta_w_words)]
         scales_dram = [phi_w_scales, theta_w_scales]
         out_rows = [out[b].rearrange("(m p) u v -> p m (u v)", p=P) for b in range(BATCHES)]
 
@@ -83,15 +82,13 @@ def tile_attgcn_pa_k_kernel(
         phi_planes = keep.tile([P, N_GROUPS // PLANES_PER_TILE, CHANNELS], U8, align_bytes=64)
         theta_planes = keep.tile([P, N_GROUPS // PLANES_PER_TILE, CHANNELS], U8, align_bytes=64)
         w_planes = [phi_planes, theta_planes]
-        late_codes = keep.tile([P, ROW_TILES - EARLY_TILES, N_ROUNDS, ROUND_WORDS], U32, align_bytes=64)
-        late_scales = keep.tile([P, ROW_TILES - EARLY_TILES, N_ROUNDS, ROUND_WORDS], U8, align_bytes=64)
         kappa_words = keep.tile([P, CHANNELS], U32, align_bytes=64)
         kappa_plane = keep.tile([P, CHANNELS], U8, align_bytes=64)
         a_bf = keep.tile([P, M_TILES, JOINTS * JOINTS], BF16)
         a_plus = keep.tile([P, M_TILES, JOINTS * JOINTS], F32)
         ident = keep.tile([P, P], F32)
-        time_sum = keep.tile([P, JOINTS], F32)
-        time_mean = keep.tile([P, JOINTS], F32)
+        pick_by_time = keep.tile([P, JOINTS], F32)
+        pick_by_joint = keep.tile([P, HALF], F32)
         lam_bf = keep.tile([P, 1], BF16)
         lam_col = keep.tile([P, 1], F32)
         kappa_b_bf = keep.tile([P, M_TILES], BF16)
@@ -99,6 +96,7 @@ def tile_attgcn_pa_k_kernel(
         phi_b_bf = keep.tile([P, PACK], BF16)
         theta_b_bf = keep.tile([P, PACK], BF16)
         bias_diff = keep.tile([P, PACK], F32)
+        bias_sum = keep.tile([P, PACK], F32)
 
         def load_scale_rows(k):
             w, s = k % 2, k // 2
@@ -111,30 +109,31 @@ def tile_attgcn_pa_k_kernel(
                 )
 
         def load_words(r):
-            groups = slice(GROUPS_PER_ROUND * r, GROUPS_PER_ROUND * (r + 1))
-            for w in range(2):
+            groups = slice(ROUND_GROUPS * r, ROUND_GROUPS * (r + 1))
+            for w in (THETA, PHI):
                 nc.sync.dma_start(out=w_words[w][:, groups, :].bitcast(I32), in_=words_dram[w][:, groups, :])
 
-        x_chunks = {}
+        x_rounds = {}
 
         def load_x(r):
-            x_chunk = x_pool.tile([P, ROW_TILES, ROUND_COLS], BF16)
-            for b in range(BATCHES):
-                tiles = slice(TILES_PER_BATCH * b, TILES_PER_BATCH * (b + 1))
-                nc.sync.dma_start(
-                    out=x_chunk[:, tiles, :], in_=x_rows[:, tiles, ROUND_COLS * r : ROUND_COLS * (r + 1)]
-                )
-            x_chunks[r] = x_chunk
-            load_scale_rows(r)
+            features = slice(ROUND_COLS * r, ROUND_COLS * (r + 1))
+            x_round = x_pool.tile([P, ROW_TILES, ROUND_COLS], BF16)
+            nc.sync.dma_start(out=x_round[:, 0:2, :], in_=x_by_time[:, 0:2, features])
+            for a in (2, 3):
+                nc.sync.dma_start(out=x_round[:, a, :], in_=x_by_joint[1, HALF * (a - 2) : HALF * (a - 1), :, features])
+            x_rounds[r] = x_round
 
         for plane in (phi_planes, theta_planes, kappa_plane):
             nc.vector.memset(plane[:].bitcast(I32), 0)
 
         load_x(0)
-        load_x(1)
-        for r in range(X_BUFS - 2):
+        load_scale_rows(0)
+        load_scale_rows(1)
+        load_words(0)
+        for r in range(1, X_BUFS):
+            load_x(r)
+            load_scale_rows(r + 1)
             load_words(r)
-            load_x(r + 2)
 
         masks.make_identity(nc, ident[:])
         nc.gpsimd.dma_start(out=lam_bf[:], in_=lam.partition_broadcast(P))
@@ -145,206 +144,275 @@ def tile_attgcn_pa_k_kernel(
         nc.gpsimd.tensor_copy(out=lam_col[:], in_=lam_bf[:])
         nc.gpsimd.tensor_tensor(out=bias_diff[:], in0=theta_b_bf[:], in1=phi_b_bf[:], op=ALU.subtract)
         nc.gpsimd.tensor_scalar(
+            out=bias_sum[:], in0=bias_diff[:], scalar1=float(TIMES), scalar2=0.0, op0=ALU.mult, op1=ALU.add
+        )
+        nc.gpsimd.tensor_scalar(
             out=lam_kappa_b[:], in0=kappa_b_bf[:], scalar1=lam_col[:, 0:1], scalar2=0.0, op0=ALU.mult, op1=ALU.add
         )
         nc.vector.tensor_reduce(
-            out=time_sum[:], in_=ident[:].rearrange("q (t u) -> q u t", u=JOINTS), axis=AXIS.X, op=ALU.add
+            out=pick_by_time[:], in_=ident[:].rearrange("q (t v) -> q v t", t=T_HALF), axis=AXIS.X, op=ALU.add
         )
-        nc.vector.tensor_scalar(out=time_mean[:], in0=time_sum[:], scalar1=1.0 / TIMES, scalar2=None, op0=ALU.mult)
+        nc.vector.tensor_reduce(
+            out=pick_by_joint[:], in_=ident[:].rearrange("q (v t) -> q v t", t=TIMES), axis=AXIS.X, op=ALU.add
+        )
 
-        x_quantised = {}
-
-        x_sorted_of = {}
+        sorted_of, grouped_of, quantised = {}, {}, {}
 
         def sort_words(r):
-            x_sorted = regroup.tile([P, ROW_TILES, GROUPS_PER_ROUND, 2, P], F32)
+            x_sorted = regroup.tile([P, BLOCKS, 2, P], F32)
             for b in range(BATCHES):
-                tiles = slice(TILES_PER_BATCH * b, TILES_PER_BATCH * (b + 1))
+                half = BLOCKS // 2
                 nc.vector.tensor_copy(
-                    out=x_sorted[:, tiles].rearrange("q a g h p -> q (a g) h p"),
-                    in_=x_chunks[r][:, tiles, :]
+                    out=x_sorted[:, half * b : half * (b + 1)],
+                    in_=x_rounds[r][:, 2 * b : 2 * b + 2, :]
+                    .rearrange("q a c -> q (a c)")
                     .bitcast(F32)
-                    .rearrange("q a (g p h) -> q (a g) h p", g=GROUPS_PER_ROUND, h=2),
+                    .rearrange("q (k p h) -> q k h p", k=half, h=2),
                 )
-            x_sorted_of[r] = x_sorted
+            sorted_of[r] = x_sorted
 
-        def transpose_and_quantise(r):
-            x_sorted = x_sorted_of[r]
-            grouped = regroup.tile([P, ROW_TILES, GROUPS_PER_ROUND, P * PACK], BF16, align_bytes=64)
-            for b in range(BATCHES):
-                tiles = slice(TILES_PER_BATCH * b, TILES_PER_BATCH * (b + 1))
-                for gi in range(GROUPS_PER_ROUND):
-                    xt = psum_work.tile([P, TILES_PER_BATCH, 2, P], F32, tag="work")
-                    for rt in range(TILES_PER_BATCH):
-                        for h in range(2):
-                            nc.tensor.transpose(
-                                xt[:, rt, h, :], x_sorted[:, TILES_PER_BATCH * b + rt, gi, h, :], ident[:]
-                            )
-                    nc.scalar.copy(
-                        out=grouped[:, tiles, gi, :].bitcast(F32).rearrange("p rt (q h) -> p rt q h", h=2),
-                        in_=xt[:].rearrange("p rt h q -> p rt q h"),
-                    )
-            x_codes = quant.tile([P, EARLY_TILES, ROUND_WORDS], U32, align_bytes=64)
-            x_scales = quant.tile([P, EARLY_TILES, ROUND_WORDS], U8, align_bytes=64)
-            for a in range(ROW_TILES):
-                if a < EARLY_TILES:
-                    x_quantised[a, r] = (x_codes[:, a, :], x_scales[:, a, :])
-                else:
-                    x_quantised[a, r] = (late_codes[:, a - EARLY_TILES, r, :], late_scales[:, a - EARLY_TILES, r, :])
-                codes, scales = x_quantised[a, r]
+        def transposes(r):
+            x_sorted = sorted_of[r]
+            grouped = regroup.tile([P, BLOCKS, P * PACK], BF16, align_bytes=64)
+            for k in range(0, BLOCKS, 2):
+                xt = psum_work.tile([P, 2, 2, P], F32, tag="work")
+                for i in range(2):
+                    for h in range(2):
+                        nc.tensor.transpose(xt[:, i, h, :], x_sorted[:, k + i, h, :], ident[:])
+                nc.scalar.copy(
+                    out=grouped[:, k : k + 2, :].bitcast(F32).rearrange("p k (q h) -> p k q h", h=2),
+                    in_=xt[:].rearrange("p k h q -> p k q h"),
+                )
+            grouped_of[r] = grouped
+
+        late_codes = keep.tile([P, N_ROUNDS, ROUND_GROUPS * P], U32, align_bytes=64)
+        late_scales = keep.tile([P, N_ROUNDS, ROUND_GROUPS * P], U8, align_bytes=64)
+
+        def quantise(r):
+            grouped = grouped_of[r]
+            codes = quant.tile([P, 3 * ROUND_GROUPS * P], U32, align_bytes=64)
+            scales = quant.tile([P, 3 * ROUND_GROUPS * P], U8, align_bytes=64)
+            n = ROUND_GROUPS
+            for a0, a1, out_codes, out_scales in (
+                (0, 2, codes[:, 0 : 2 * n * P], scales[:, 0 : 2 * n * P]),
+                (2, 3, codes[:, 2 * n * P : 3 * n * P], scales[:, 2 * n * P : 3 * n * P]),
+                (3, 4, late_codes[:, r, :], late_scales[:, r, :]),
+            ):
                 nc.vector.quantize_mx(
-                    out=codes.bitcast(FP8X4), scales=scales, in_=grouped[:, a].rearrange("p g c -> p (g c)")
+                    out=out_codes.bitcast(FP8X4),
+                    scales=out_scales,
+                    in_=grouped[:, n * a0 : n * a1, :].rearrange("p k c -> p (k c)"),
                 )
+            quantised[r] = (codes, scales)
 
-        sums = []
-        for b in range(BATCHES):
-            acc_phi = psum_acc.tile([P, CHANNELS], F32)
-            acc_theta = psum_acc.tile([P, CHANNELS], F32)
-            sums.append([acc_phi, acc_theta])
+        sums = {}
 
-        def multiply(r, row_tiles):
-            for gi in range(GROUPS_PER_ROUND):
-                g = GROUPS_PER_ROUND * r + gi
-                s, plane_start = g // PLANES_PER_TILE, 4 * (g % PLANES_PER_TILE)
-                rows = slice(gi * P, (gi + 1) * P)
-                for a in row_tiles:
-                    b, rt = divmod(a, TILES_PER_BATCH)
-                    codes, scales = x_quantised[a, r]
-                    for w in range(2):
+        def multiply(r, tiles, weights):
+            for w in weights:
+                for a in tiles:
+                    s = max(a - 1, 0)
+                    for gi in range(ROUND_GROUPS):
+                        g = ROUND_GROUPS * r + gi
+                        if a < 3:
+                            codes, scales = quantised[r]
+                            rows = slice(P * (a * ROUND_GROUPS + gi), P * (a * ROUND_GROUPS + gi + 1))
+                            lhs, lhs_scale = codes[:, rows], scales[:, rows]
+                        else:
+                            rows = slice(P * gi, P * (gi + 1))
+                            lhs, lhs_scale = late_codes[:, r, rows], late_scales[:, r, rows]
+                        first = g == 0 and a != 1
+                        if first:
+                            bank = psum_acc.tile([P, CHANNELS], F32, tag="acc")
+                            sums[s, w] = bank
+                        block, plane_start = g // PLANES_PER_TILE, 4 * (g % PLANES_PER_TILE)
                         nc.tensor.matmul_mx(
-                            out=sums[b][w][:],
-                            lhsT=codes[:, rows].bitcast(FP8X4),
-                            lhsT_scale=scales[:, rows],
+                            out=sums[s, w][:],
+                            lhsT=lhs.bitcast(FP8X4),
+                            lhsT_scale=lhs_scale,
                             rhs=w_words[w][:, g, :].bitcast(FP8X4),
-                            rhs_scale=w_planes[w][plane_start:P, s, :],
-                            start=(g == 0 and rt == 0),
-                            stop=(g == N_GROUPS - 1 and rt == TILES_PER_BATCH - 1),
+                            rhs_scale=w_planes[w][plane_start:P, block, :],
+                            start=first,
+                            stop=(g == N_GROUPS - 1 and a != 0),
                         )
 
-        held = {}
+        y_of, turned_of, p_of, th_of, held = {}, {}, {}, {}, {}
+        for b in range(BATCHES):
+            p_sums = keep.tile([P, JOINTS, PACK], F32, name="p%d" % b)
+            th_sums = keep.tile([P, JOINTS, PACK], F32, name="th%d" % b)
+            p_of[b], th_of[b] = p_sums, th_sums
 
-        def sums_leave_psum(b):
-            y_phi = once.tile([P, PACK, P], F32)
-            y_theta = once.tile([P, PACK, P], F32)
-            held["y"] = [y_phi, y_theta]
-            for w in range(2):
-                nc.scalar.copy(out=held["y"][w][:], in_=sums[b][w][:].rearrange("q (p j) -> q j p", j=PACK))
+        def leave_psum(s, w):
+            y = keep.tile([P, PACK, P], F32, name="y%d%d" % (s, w))
+            nc.scalar.copy(out=y[:], in_=sums[s, w][:].rearrange("q (p j) -> q j p", j=PACK))
+            y_of[s, w] = y
 
-        def joint_means(b):
-            means = psum_means.tile([P, 2, PACK, JOINTS], F32)
-            for w in range(2):
-                for j in range(PACK):
-                    nc.tensor.matmul(
-                        means[:, w, j, :], lhsT=held["y"][w][:, j, :], rhs=time_mean[:], start=True, stop=True
-                    )
-            th = once.tile([P, JOINTS, PACK], F32)
-            nc.vector.tensor_tensor(
-                out=th[:],
-                in0=means[:, 1].rearrange("p j v -> p v j"),
-                in1=bias_diff[:].unsqueeze(1).to_broadcast([P, JOINTS, PACK]),
+        def turn(s, w):
+            pool, tag = (psum_work, "work") if s == 0 else (psum_acc, "acc")
+            turned = pool.tile([P, PACK, P], F32, tag=tag)
+            for j in range(PACK):
+                nc.tensor.transpose(turned[:, j, :], y_of[s, w][:, j, :], ident[:])
+            turned_of[s, w] = turned
+
+        def sum_over_time(s, w):
+            b, v0, n = (0, 0, JOINTS) if s == 0 else (1, HALF * (s - 1), HALF)
+            rows = "(t v)" if s == 0 else "(v t)"
+            target = (p_of if w == PHI else th_of)[b][:, v0 : v0 + n, :]
+            nc.vector.tensor_reduce(
+                out=target,
+                in_=turned_of[s, w][:].rearrange("p j %s -> p v j t" % rows, v=n),
+                axis=AXIS.X,
                 op=ALU.add,
             )
-            held["means"], held["th"] = means, th
+            if w == THETA:
+                nc.vector.tensor_tensor(
+                    out=target, in0=target, in1=bias_sum[:].unsqueeze(1).to_broadcast([P, n, PACK]), op=ALU.add
+                )
 
         def differences(b, c):
             shape = [P, U_CHUNK, JOINTS, PACK]
             d = twice.tile(shape, F32)
             nc.vector.tensor_tensor(
                 out=d[:],
-                in0=held["means"][:, 0, :, U_CHUNK * c : U_CHUNK * (c + 1)]
-                .rearrange("p j u -> p u j")
-                .unsqueeze(2)
-                .to_broadcast(shape),
-                in1=held["th"][:].unsqueeze(1).to_broadcast(shape),
+                in0=p_of[b][:, U_CHUNK * c : U_CHUNK * (c + 1), :].unsqueeze(2).to_broadcast(shape),
+                in1=th_of[b][:].unsqueeze(1).to_broadcast(shape),
                 op=ALU.subtract,
             )
-            held["d", c] = d
+            held["d", b, c] = d
 
         def tanh(b, c):
             f = twice.tile([P, CHUNK_COLS * PACK], BF16, align_bytes=64)
-            nc.scalar.activation(out=f[:], in_=held["d", c][:].rearrange("p u v j -> p (u v j)"), func=ACT.Tanh)
-            held["f", c] = f
+            nc.scalar.activation(
+                out=f[:], in_=held["d", b, c][:].rearrange("p u v j -> p (u v j)"), func=ACT.Tanh, scale=1.0 / TIMES
+            )
+            held["f", b, c] = f
 
-        def outputs(b, c):
+        def quantise_f(b, c):
             f_codes = twice.tile([P, CHUNK_COLS], U32, align_bytes=64)
             f_scales = twice.tile([P, CHUNK_COLS], U8, align_bytes=64)
-            nc.vector.quantize_mx(out=f_codes[:].bitcast(FP8X4), scales=f_scales[:], in_=held["f", c][:])
+            nc.vector.quantize_mx(out=f_codes[:].bitcast(FP8X4), scales=f_scales[:], in_=held["f", b, c][:])
+            held["q", b, c] = (f_codes, f_scales)
+
+        def products(b, c):
+            f_codes, f_scales = held["q", b, c]
+            for pair in range(M_TILES // 2):
+                g_ps = psum_work.tile([P, 2, CHUNK_COLS], F32, tag="work")
+                for i in range(2):
+                    channels = slice(P * (2 * pair + i), P * (2 * pair + i + 1))
+                    nc.tensor.matmul_mx(
+                        out=g_ps[:, i, :],
+                        lhsT=kappa_words[:, channels].bitcast(FP8X4),
+                        lhsT_scale=kappa_plane[:, channels],
+                        rhs=f_codes[:].bitcast(FP8X4),
+                        rhs_scale=f_scales[:],
+                        start=True,
+                        stop=True,
+                    )
+                held["g", b, c, pair] = g_ps
+
+        def add_bias_to_a(m):
+            nc.vector.tensor_scalar(
+                out=a_plus[:, m, :], in0=a_bf[:, m, :], scalar1=lam_kappa_b[:, m : m + 1], scalar2=None, op0=ALU.add
+            )
+
+        def finish(b, c, pair):
             cols = slice(CHUNK_COLS * c, CHUNK_COLS * (c + 1))
-            for m in range(M_TILES):
-                channels = slice(P * m, P * (m + 1))
-                g_ps = psum_work.tile([P, CHUNK_COLS], F32, tag="work")
-                nc.tensor.matmul_mx(
-                    out=g_ps[:],
-                    lhsT=kappa_words[:, channels].bitcast(FP8X4),
-                    lhsT_scale=kappa_plane[:, channels],
-                    rhs=f_codes[:].bitcast(FP8X4),
-                    rhs_scale=f_scales[:],
-                    start=True,
-                    stop=True,
-                )
-                result = results.tile([P, CHUNK_COLS], F32)
+            g_ps = held["g", b, c, pair]
+            result = results.tile([P, 2, CHUNK_COLS], F32)
+            ms = slice(2 * pair, 2 * pair + 2)
+            if pair == 1 and b * N_CHUNKS + c in BY_SCALAR:
+                scaled = twice.tile([P, 2, CHUNK_COLS], F32)
+                nc.scalar.activation(out=scaled[:], in_=g_ps[:], func=ACT.Copy, scale=lam_col[:, 0:1])
+                nc.gpsimd.tensor_tensor(out=result[:], in0=scaled[:], in1=a_plus[:, ms, cols], op=ALU.add)
+            else:
                 nc.vector.scalar_tensor_tensor(
-                    out=result[:],
-                    in0=g_ps[:],
-                    scalar=lam_col[:, 0:1],
-                    in1=a_plus[:, m, cols],
-                    op0=ALU.mult,
-                    op1=ALU.add,
+                    out=result[:], in0=g_ps[:], scalar=lam_col[:, 0:1], in1=a_plus[:, ms, cols], op0=ALU.mult, op1=ALU.add
                 )
-                nc.sync.dma_start(out=out_rows[b][:, m, cols], in_=result[:])
+            nc.sync.dma_start(out=out_rows[b][:, ms, cols], in_=result[:])
 
-        def chunk_step(b, s):
-            if 0 <= s - 1 < N_CHUNKS:
-                tanh(b, s - 1)
-            if s < N_CHUNKS:
-                differences(b, s)
-            if 0 <= s - 2:
-                outputs(b, s - 2)
+        def load_rest():
+            for pair in range(M_TILES // 2):
+                nc.sync.dma_start(
+                    out=a_bf[:, 2 * pair : 2 * pair + 2, :],
+                    in_=A.rearrange("(m p) u v -> p m (u v)", p=P)[:, 2 * pair : 2 * pair + 2, :],
+                )
+            nc.sync.dma_start(
+                out=kappa_words[:].bitcast(I32), in_=kappa_w_words[0].rearrange("p n t -> p (n t)").bitcast(I32)
+            )
+            for quadrant in range(QUADRANTS):
+                nc.sync.dma_start(
+                    out=kappa_plane[32 * quadrant : 32 * quadrant + 4, :].bitcast(I32),
+                    in_=kappa_w_scales[0, 4 * quadrant : 4 * quadrant + 4, :].bitcast(I32),
+                )
 
-        n_steps = N_CHUNKS + 2
-
+        BOTH = (THETA, PHI)
         sort_words(0)
+        transposes(0)
+        quantise(0)
         sort_words(1)
-        transpose_and_quantise(0)
         for r in range(N_ROUNDS):
+            multiply(r, (0, 1), BOTH)
+            if r + 1 < N_ROUNDS:
+                transposes(r + 1)
+                quantise(r + 1)
             if r + 2 < N_ROUNDS:
                 sort_words(r + 2)
-            if r + 1 < N_ROUNDS:
-                transpose_and_quantise(r + 1)
-            if r + X_BUFS - 2 < N_ROUNDS:
-                load_words(r + X_BUFS - 2)
             if r + X_BUFS < N_ROUNDS:
                 load_x(r + X_BUFS)
-            multiply(r, range(EARLY_TILES))
+                if r + X_BUFS + 1 < N_ROUNDS:
+                    load_scale_rows(r + X_BUFS + 1)
+                load_words(r + X_BUFS)
+            if r + X_BUFS == N_ROUNDS:
+                load_rest()
+            if r == N_ROUNDS - 1:
+                leave_psum(0, THETA)
+                leave_psum(0, PHI)
+                add_bias_to_a(0)
+                add_bias_to_a(1)
+                turn(0, THETA)
+                turn(0, PHI)
+                sum_over_time(0, THETA)
+                sum_over_time(0, PHI)
+            elif r >= LAG:
+                multiply(r - LAG, (2,), BOTH)
 
-        nc.sync.dma_start(
-            out=kappa_words[:].bitcast(I32), in_=kappa_w_words[0].rearrange("p n t -> p (n t)").bitcast(I32)
-        )
-        for quadrant in range(QUADRANTS):
-            nc.sync.dma_start(
-                out=kappa_plane[32 * quadrant : 32 * quadrant + 4, :].bitcast(I32),
-                in_=kappa_w_scales[0, 4 * quadrant : 4 * quadrant + 4, :].bitcast(I32),
-            )
-        nc.sync.dma_start(out=a_bf[:], in_=A.rearrange("(m p) u v -> p m (u v)", p=P))
-        for m in range(M_TILES):
-            nc.gpsimd.tensor_scalar(
-                out=a_plus[:, m, :],
-                in0=a_bf[:, m, :],
-                scalar1=1.0,
-                scalar2=lam_kappa_b[:, m : m + 1],
-                op0=ALU.mult,
-                op1=ALU.add,
-            )
-
-        rounds_per_step = N_ROUNDS // n_steps
-        sums_leave_psum(0)
-        joint_means(0)
-        for s in range(n_steps):
-            for r in range(rounds_per_step * s, rounds_per_step * (s + 1)):
-                multiply(r, range(EARLY_TILES, ROW_TILES))
-            if s == n_steps - 1:
-                sums_leave_psum(1)
-            chunk_step(0, s)
-        joint_means(1)
-        for s in range(n_steps):
-            chunk_step(1, s)
+        late = [(r, (2,), BOTH) for r in range(N_ROUNDS - 1 - LAG, N_ROUNDS)]
+        late += [(r, (3,), (THETA,)) for r in range(N_ROUNDS)] + [(r, (3,), (PHI,)) for r in range(N_ROUNDS)]
+        chunks = [(0, c) for c in range(N_CHUNKS)] + [None] * 0 + [(1, c) for c in range(N_CHUNKS)] + [None] * 3
+        done = 0
+        for s in range(len(chunks)):
+            now, before, third, fourth = [chunks[s - i] if s >= i else None for i in range(4)]
+            if third:
+                quantise_f(*third)
+                products(*third)
+            if fourth:
+                finish(*fourth, 0)
+                finish(*fourth, 1)
+            if s == 6:
+                turn(2, PHI)
+                sum_over_time(2, PHI)
+            if now == (1, 0):
+                sum_over_time(1, THETA)
+                sum_over_time(1, PHI)
+                sum_over_time(2, THETA)
+            if now:
+                differences(*now)
+            if before:
+                tanh(*before)
+            if s == 1:
+                add_bias_to_a(2)
+                add_bias_to_a(3)
+                leave_psum(1, THETA)
+                leave_psum(1, PHI)
+            if s == 3:
+                leave_psum(2, THETA)
+            if s == 6 - 1:
+                leave_psum(2, PHI)
+            upto = min(len(late), (1, 5, 9, 13, 17)[min(s, 4)])
+            for item in late[done:upto]:
+                multiply(*item)
+            done = upto
+            if s == 1:
+                turn(1, THETA)
+                turn(1, PHI)
+            if s == 3:
+                turn(2, THETA)

@@ -21,7 +21,6 @@ PLANES_PER_TILE = 4
 
 BATCHES, TIMES, JOINTS, FEATURES, CHANNELS = 2, 8, 32, 8192, 512
 T_HALF = TIMES // 2
-HALF = JOINTS // 2
 ROW_TILES = 2 * BATCHES
 N_GROUPS = FEATURES // GROUP
 PHI, THETA = 0, 1
@@ -71,7 +70,6 @@ def tile_attgcn_pa_k_kernel(
         psum_work = ctx.enter_context(tc.psum_pool(name="psum_work", bufs=4))
 
         x_by_time = x.rearrange("b (rt t) v c -> (t v) (b rt) c", t=T_HALF)
-        x_by_joint = x.rearrange("b t v c -> b v t c")
         words_dram = [w.rearrange("g p n t -> p g (n t)").bitcast(I32) for w in (phi_w_words, theta_w_words)]
         scales_dram = [phi_w_scales, theta_w_scales]
         out_rows = [out[b].rearrange("(m p) u v -> p m (u v)", p=P) for b in range(BATCHES)]
@@ -87,8 +85,6 @@ def tile_attgcn_pa_k_kernel(
         a_bf = keep.tile([P, M_TILES, JOINTS * JOINTS], BF16)
         a_plus = keep.tile([P, M_TILES, JOINTS * JOINTS], F32)
         ident = keep.tile([P, P], F32)
-        pick_by_time = keep.tile([P, JOINTS], F32)
-        pick_by_joint = keep.tile([P, HALF], F32)
         lam_bf = keep.tile([P, 1], BF16)
         lam_col = keep.tile([P, 1], F32)
         kappa_b_bf = keep.tile([P, M_TILES], BF16)
@@ -118,9 +114,8 @@ def tile_attgcn_pa_k_kernel(
         def load_x(r):
             features = slice(ROUND_COLS * r, ROUND_COLS * (r + 1))
             x_round = x_pool.tile([P, ROW_TILES, ROUND_COLS], BF16)
-            nc.sync.dma_start(out=x_round[:, 0:2, :], in_=x_by_time[:, 0:2, features])
-            for a in (2, 3):
-                nc.sync.dma_start(out=x_round[:, a, :], in_=x_by_joint[1, HALF * (a - 2) : HALF * (a - 1), :, features])
+            for b in range(BATCHES):
+                nc.sync.dma_start(out=x_round[:, 2 * b : 2 * b + 2, :], in_=x_by_time[:, 2 * b : 2 * b + 2, features])
             x_rounds[r] = x_round
 
         for plane in (phi_planes, theta_planes, kappa_plane):
@@ -148,12 +143,6 @@ def tile_attgcn_pa_k_kernel(
         )
         nc.gpsimd.tensor_scalar(
             out=lam_kappa_b[:], in0=kappa_b_bf[:], scalar1=lam_col[:, 0:1], scalar2=0.0, op0=ALU.mult, op1=ALU.add
-        )
-        nc.vector.tensor_reduce(
-            out=pick_by_time[:], in_=ident[:].rearrange("q (t v) -> q v t", t=T_HALF), axis=AXIS.X, op=ALU.add
-        )
-        nc.vector.tensor_reduce(
-            out=pick_by_joint[:], in_=ident[:].rearrange("q (v t) -> q v t", t=TIMES), axis=AXIS.X, op=ALU.add
         )
 
         sorted_of, grouped_of, quantised = {}, {}, {}
@@ -210,7 +199,7 @@ def tile_attgcn_pa_k_kernel(
         def multiply(r, tiles, weights):
             for w in weights:
                 for a in tiles:
-                    s = max(a - 1, 0)
+                    s, rt = divmod(a, 2)
                     for gi in range(ROUND_GROUPS):
                         g = ROUND_GROUPS * r + gi
                         if a < 3:
@@ -220,7 +209,7 @@ def tile_attgcn_pa_k_kernel(
                         else:
                             rows = slice(P * gi, P * (gi + 1))
                             lhs, lhs_scale = late_codes[:, r, rows], late_scales[:, r, rows]
-                        first = g == 0 and a != 1
+                        first = g == 0 and rt == 0
                         if first:
                             bank = psum_acc.tile([P, CHANNELS], F32, tag="acc")
                             sums[s, w] = bank
@@ -232,7 +221,7 @@ def tile_attgcn_pa_k_kernel(
                             rhs=w_words[w][:, g, :].bitcast(FP8X4),
                             rhs_scale=w_planes[w][plane_start:P, block, :],
                             start=first,
-                            stop=(g == N_GROUPS - 1 and a != 0),
+                            stop=(g == N_GROUPS - 1 and rt == 1),
                         )
 
         y_of, turned_of, p_of, th_of, held = {}, {}, {}, {}, {}
@@ -254,18 +243,16 @@ def tile_attgcn_pa_k_kernel(
             turned_of[s, w] = turned
 
         def sum_over_time(s, w):
-            b, v0, n = (0, 0, JOINTS) if s == 0 else (1, HALF * (s - 1), HALF)
-            rows = "(t v)" if s == 0 else "(v t)"
-            target = (p_of if w == PHI else th_of)[b][:, v0 : v0 + n, :]
+            target = (p_of if w == PHI else th_of)[s][:]
             nc.vector.tensor_reduce(
                 out=target,
-                in_=turned_of[s, w][:].rearrange("p j %s -> p v j t" % rows, v=n),
+                in_=turned_of[s, w][:].rearrange("p j (t v) -> p v j t", t=T_HALF),
                 axis=AXIS.X,
                 op=ALU.add,
             )
             if w == THETA:
                 nc.vector.tensor_tensor(
-                    out=target, in0=target, in1=bias_sum[:].unsqueeze(1).to_broadcast([P, n, PACK]), op=ALU.add
+                    out=target, in0=target, in1=bias_sum[:].unsqueeze(1).to_broadcast([P, JOINTS, PACK]), op=ALU.add
                 )
 
         def differences(b, c):
@@ -377,7 +364,7 @@ def tile_attgcn_pa_k_kernel(
 
         late = [(r, (2,), BOTH) for r in range(N_ROUNDS - 1 - LAG, N_ROUNDS)]
         late += [(r, (3,), (THETA,)) for r in range(N_ROUNDS)] + [(r, (3,), (PHI,)) for r in range(N_ROUNDS)]
-        chunks = [(0, c) for c in range(N_CHUNKS)] + [None] * 0 + [(1, c) for c in range(N_CHUNKS)] + [None] * 3
+        chunks = [(0, c) for c in range(N_CHUNKS)] + [None] * 1 + [(1, c) for c in range(N_CHUNKS)] + [None] * 3
         done = 0
         for s in range(len(chunks)):
             now, before, third, fourth = [chunks[s - i] if s >= i else None for i in range(4)]
@@ -387,13 +374,9 @@ def tile_attgcn_pa_k_kernel(
             if fourth:
                 finish(*fourth, 0)
                 finish(*fourth, 1)
-            if s == 6:
-                turn(2, PHI)
-                sum_over_time(2, PHI)
             if now == (1, 0):
                 sum_over_time(1, THETA)
                 sum_over_time(1, PHI)
-                sum_over_time(2, THETA)
             if now:
                 differences(*now)
             if before:
@@ -401,18 +384,15 @@ def tile_attgcn_pa_k_kernel(
             if s == 1:
                 add_bias_to_a(2)
                 add_bias_to_a(3)
+            if s == 2:
                 leave_psum(1, THETA)
+            if s == 4:
                 leave_psum(1, PHI)
-            if s == 3:
-                leave_psum(2, THETA)
-            if s == 6 - 1:
-                leave_psum(2, PHI)
-            upto = min(len(late), (1, 5, 9, 13, 17)[min(s, 4)])
+            upto = min(len(late), (3, 9, 13, 17)[min(s, 3)])
             for item in late[done:upto]:
                 multiply(*item)
             done = upto
-            if s == 1:
+            if s == 2:
                 turn(1, THETA)
+            if s == 4:
                 turn(1, PHI)
-            if s == 3:
-                turn(2, THETA)

@@ -36,7 +36,8 @@ U_CHUNK = 8
 N_CHUNKS = JOINTS // U_CHUNK
 CHUNK_COLS = U_CHUNK * JOINTS
 M_TILES = CHANNELS // P
-BY_SCALAR = ()
+EARLY_THETA = 5
+BY_SCALAR = range(7)
 
 FLOPS = 2 * BATCHES * TIMES * JOINTS * FEATURES * 2 * CHANNELS + 2 * BATCHES * JOINTS * JOINTS * CHANNELS * CHANNELS
 
@@ -85,6 +86,7 @@ def tile_attgcn_pa_k_kernel(
         a_bf = keep.tile([P, M_TILES, JOINTS * JOINTS], BF16)
         a_plus = keep.tile([P, M_TILES, JOINTS * JOINTS], F32)
         ident = keep.tile([P, P], F32)
+        pick_joint = keep.tile([P, JOINTS], F32)
         lam_bf = keep.tile([P, 1], BF16)
         lam_col = keep.tile([P, 1], F32)
         kappa_b_bf = keep.tile([P, M_TILES], BF16)
@@ -143,6 +145,10 @@ def tile_attgcn_pa_k_kernel(
         )
         nc.gpsimd.tensor_scalar(
             out=lam_kappa_b[:], in0=kappa_b_bf[:], scalar1=lam_col[:, 0:1], scalar2=0.0, op0=ALU.mult, op1=ALU.add
+        )
+
+        nc.vector.tensor_reduce(
+            out=pick_joint[:], in_=ident[:].rearrange("q (t v) -> q v t", t=T_HALF), axis=AXIS.X, op=ALU.add
         )
 
         sorted_of, grouped_of, quantised = {}, {}, {}
@@ -226,41 +232,44 @@ def tile_attgcn_pa_k_kernel(
 
         y_of, turned_of, p_of, th_of, held = {}, {}, {}, {}, {}
         for b in range(BATCHES):
-            p_sums = keep.tile([P, JOINTS, PACK], F32, name="p%d" % b)
             th_sums = keep.tile([P, JOINTS, PACK], F32, name="th%d" % b)
-            p_of[b], th_of[b] = p_sums, th_sums
+            th_of[b] = th_sums
 
         def leave_psum(s, w):
             y = keep.tile([P, PACK, P], F32, name="y%d%d" % (s, w))
             nc.scalar.copy(out=y[:], in_=sums[s, w][:].rearrange("q (p j) -> q j p", j=PACK))
             y_of[s, w] = y
 
-        def turn(s, w):
-            pool, tag = (psum_work, "work") if s == 0 else (psum_acc, "acc")
-            turned = pool.tile([P, PACK, P], F32, tag=tag)
+        def turn(b, w):
+            if w == PHI:
+                means = psum_acc.tile([P, PACK, JOINTS], F32, tag="acc")
+                for j in range(PACK):
+                    nc.tensor.matmul(means[:, j, :], lhsT=y_of[b, w][:, j, :], rhs=pick_joint[:], start=True, stop=True)
+                p_of[b] = means
+                return
+            turned = psum_work.tile([P, PACK, P], F32, tag="work")
             for j in range(PACK):
-                nc.tensor.transpose(turned[:, j, :], y_of[s, w][:, j, :], ident[:])
-            turned_of[s, w] = turned
+                nc.tensor.transpose(turned[:, j, :], y_of[b, w][:, j, :], ident[:])
+            turned_of[b] = turned
 
-        def sum_over_time(s, w):
-            target = (p_of if w == PHI else th_of)[s][:]
+        def sum_over_time(b):
+            th = th_of[b]
             nc.vector.tensor_reduce(
-                out=target,
-                in_=turned_of[s, w][:].rearrange("p j (t v) -> p v j t", t=T_HALF),
-                axis=AXIS.X,
-                op=ALU.add,
+                out=th[:], in_=turned_of[b][:].rearrange("p j (t v) -> p v j t", t=T_HALF), axis=AXIS.X, op=ALU.add
             )
-            if w == THETA:
-                nc.vector.tensor_tensor(
-                    out=target, in0=target, in1=bias_sum[:].unsqueeze(1).to_broadcast([P, JOINTS, PACK]), op=ALU.add
-                )
+            nc.vector.tensor_tensor(
+                out=th[:], in0=th[:], in1=bias_sum[:].unsqueeze(1).to_broadcast([P, JOINTS, PACK]), op=ALU.add
+            )
 
         def differences(b, c):
             shape = [P, U_CHUNK, JOINTS, PACK]
             d = twice.tile(shape, F32)
             nc.vector.tensor_tensor(
                 out=d[:],
-                in0=p_of[b][:, U_CHUNK * c : U_CHUNK * (c + 1), :].unsqueeze(2).to_broadcast(shape),
+                in0=p_of[b][:, :, U_CHUNK * c : U_CHUNK * (c + 1)]
+                .rearrange("p j u -> p u j")
+                .unsqueeze(2)
+                .to_broadcast(shape),
                 in1=th_of[b][:].unsqueeze(1).to_broadcast(shape),
                 op=ALU.subtract,
             )
@@ -297,6 +306,11 @@ def tile_attgcn_pa_k_kernel(
                 held["g", b, c, pair] = g_ps
 
         def add_bias_to_a(m):
+            if m >= 2:
+                nc.scalar.activation(
+                    out=a_plus[:, m, :], in_=a_bf[:, m, :], func=ACT.Identity, bias=lam_kappa_b[:, m : m + 1]
+                )
+                return
             nc.vector.tensor_scalar(
                 out=a_plus[:, m, :], in0=a_bf[:, m, :], scalar1=lam_kappa_b[:, m : m + 1], scalar2=None, op0=ALU.add
             )
@@ -353,18 +367,19 @@ def tile_attgcn_pa_k_kernel(
             if r == N_ROUNDS - 1:
                 leave_psum(0, THETA)
                 leave_psum(0, PHI)
-                add_bias_to_a(0)
-                add_bias_to_a(1)
+                for m in range(M_TILES):
+                    add_bias_to_a(m)
                 turn(0, THETA)
                 turn(0, PHI)
-                sum_over_time(0, THETA)
-                sum_over_time(0, PHI)
+                sum_over_time(0)
             elif r >= LAG:
                 multiply(r - LAG, (2,), BOTH)
+            if r < EARLY_THETA:
+                multiply(r, (3,), (THETA,))
 
         late = [(r, (2,), BOTH) for r in range(N_ROUNDS - 1 - LAG, N_ROUNDS)]
-        late += [(r, (3,), (THETA,)) for r in range(N_ROUNDS)] + [(r, (3,), (PHI,)) for r in range(N_ROUNDS)]
-        chunks = [(0, c) for c in range(N_CHUNKS)] + [None] * 1 + [(1, c) for c in range(N_CHUNKS)] + [None] * 3
+        late += [(r, (3,), (THETA,)) for r in range(EARLY_THETA, N_ROUNDS)] + [(r, (3,), (PHI,)) for r in range(N_ROUNDS)]
+        chunks = [(0, c) for c in range(N_CHUNKS)] + [None] * 0 + [(1, c) for c in range(N_CHUNKS)] + [None] * 3
         done = 0
         for s in range(len(chunks)):
             now, before, third, fourth = [chunks[s - i] if s >= i else None for i in range(4)]
@@ -375,24 +390,20 @@ def tile_attgcn_pa_k_kernel(
                 finish(*fourth, 0)
                 finish(*fourth, 1)
             if now == (1, 0):
-                sum_over_time(1, THETA)
-                sum_over_time(1, PHI)
+                sum_over_time(1)
             if now:
                 differences(*now)
             if before:
                 tanh(*before)
             if s == 1:
-                add_bias_to_a(2)
-                add_bias_to_a(3)
-            if s == 2:
                 leave_psum(1, THETA)
-            if s == 4:
+            if s == 3:
                 leave_psum(1, PHI)
-            upto = min(len(late), (3, 9, 13, 17)[min(s, 3)])
+            upto = min(len(late), (4, 8, 12)[min(s, 2)])
             for item in late[done:upto]:
                 multiply(*item)
             done = upto
-            if s == 2:
+            if s == 1:
                 turn(1, THETA)
-            if s == 4:
+            if s == 3:
                 turn(1, PHI)

@@ -29,13 +29,15 @@ ROUND_GROUPS = 2
 N_ROUNDS = N_GROUPS // ROUND_GROUPS
 ROUND_COLS = ROUND_GROUPS * GROUP
 BLOCKS = ROW_TILES * ROUND_GROUPS
-X_BUFS = 3
 LAG = 0
 
 U_CHUNK = 8
 N_CHUNKS = JOINTS // U_CHUNK
 CHUNK_COLS = U_CHUNK * JOINTS
 M_TILES = CHANNELS // P
+TURN = 1
+AHEAD = 3
+X_BEFORE = [[(0, 0, 1), (1, 0, 1)], [(0, 1, 1), (1, 1, 1), (0, 2, 1), (1, 2, 1)], [(0, 3, 1), (1, 3, 1)], [(0, 4, 1), (1, 4, 1)], [(0, 5, 1), (1, 5, 1)], [(0, 6, 1), (1, 6, 1)], [(0, 7, 1), (1, 7, 1)], []]
 EARLY_THETA = 5
 BY_SCALAR = range(7)
 
@@ -62,9 +64,9 @@ def tile_attgcn_pa_k_kernel(
     with ExitStack() as ctx:
         ctx.enter_context(tc.manual_schedule())
         keep = ctx.enter_context(tc.tile_pool(name="keep", bufs=1))
-        x_pool = ctx.enter_context(tc.tile_pool(name="x_pool", bufs=X_BUFS))
+        x_pool = ctx.enter_context(tc.tile_pool(name="x_pool", bufs=2))
         regroup = ctx.enter_context(tc.tile_pool(name="regroup", bufs=2))
-        quant = ctx.enter_context(tc.tile_pool(name="quant", bufs=LAG + 2))
+        quant = ctx.enter_context(tc.tile_pool(name="quant", bufs=3))
         twice = ctx.enter_context(tc.tile_pool(name="twice", bufs=2))
         results = ctx.enter_context(tc.tile_pool(name="results", bufs=6))
         psum_acc = ctx.enter_context(tc.psum_pool(name="psum_acc", bufs=4))
@@ -113,24 +115,27 @@ def tile_attgcn_pa_k_kernel(
 
         x_rounds = {}
 
-        def load_x(r):
-            features = slice(ROUND_COLS * r, ROUND_COLS * (r + 1))
-            x_round = x_pool.tile([P, ROW_TILES, ROUND_COLS], BF16)
-            for b in range(BATCHES):
-                nc.sync.dma_start(out=x_round[:, 2 * b : 2 * b + 2, :], in_=x_by_time[:, 2 * b : 2 * b + 2, features])
-            x_rounds[r] = x_round
+        def load_x(b, first, n):
+            features = slice(ROUND_COLS * first, ROUND_COLS * (first + n))
+            x_chunk = x_pool.tile([P, 2, n * ROUND_COLS], BF16, tag="x%d%d" % (b, n))
+            nc.sync.dma_start(out=x_chunk[:], in_=x_by_time[:, 2 * b : 2 * b + 2, features])
+            for i in range(n):
+                x_rounds[b, first + i] = x_chunk[:, :, ROUND_COLS * i : ROUND_COLS * (i + 1)]
+
+        def load_round(r):
+            for b, first, n in X_BEFORE[r]:
+                load_x(b, first, n)
+            if r == 0:
+                load_scale_rows(0)
+                load_scale_rows(1)
+            elif r + 1 < N_ROUNDS:
+                load_scale_rows(r + 1)
+            load_words(r)
 
         for plane in (phi_planes, theta_planes, kappa_plane):
             nc.vector.memset(plane[:].bitcast(I32), 0)
-
-        load_x(0)
-        load_scale_rows(0)
-        load_scale_rows(1)
-        load_words(0)
-        for r in range(1, X_BUFS):
-            load_x(r)
-            load_scale_rows(r + 1)
-            load_words(r)
+        for r in range(AHEAD):
+            load_round(r)
 
         masks.make_identity(nc, ident[:])
         nc.gpsimd.dma_start(out=lam_bf[:], in_=lam.partition_broadcast(P))
@@ -155,14 +160,11 @@ def tile_attgcn_pa_k_kernel(
 
         def sort_words(r):
             x_sorted = regroup.tile([P, BLOCKS, 2, P], F32)
+            half = BLOCKS // 2
             for b in range(BATCHES):
-                half = BLOCKS // 2
                 nc.vector.tensor_copy(
-                    out=x_sorted[:, half * b : half * (b + 1)],
-                    in_=x_rounds[r][:, 2 * b : 2 * b + 2, :]
-                    .rearrange("q a c -> q (a c)")
-                    .bitcast(F32)
-                    .rearrange("q (k p h) -> q k h p", k=half, h=2),
+                    out=x_sorted[:, half * b : half * (b + 1)].rearrange("q (a g) h p -> q a g h p", a=2),
+                    in_=x_rounds[b, r].bitcast(F32).rearrange("q a (g p h) -> q a g h p", g=ROUND_GROUPS, h=2),
                 )
             sorted_of[r] = x_sorted
 
@@ -346,23 +348,29 @@ def tile_attgcn_pa_k_kernel(
                 )
 
         BOTH = (THETA, PHI)
-        sort_words(0)
-        transposes(0)
-        quantise(0)
-        sort_words(1)
-        for r in range(N_ROUNDS):
-            multiply(r, (0, 1), BOTH)
+        def prepare(r):
+            if r < N_ROUNDS:
+                transposes(r)
+                quantise(r)
             if r + 1 < N_ROUNDS:
-                transposes(r + 1)
-                quantise(r + 1)
-            if r + 2 < N_ROUNDS:
-                sort_words(r + 2)
-            if r + X_BUFS < N_ROUNDS:
-                load_x(r + X_BUFS)
-                if r + X_BUFS + 1 < N_ROUNDS:
-                    load_scale_rows(r + X_BUFS + 1)
-                load_words(r + X_BUFS)
-            if r + X_BUFS == N_ROUNDS:
+                sort_words(r + 1)
+
+        sort_words(0)
+        prepare(0)
+        for r in range(N_ROUNDS):
+            if r < TURN:
+                multiply(r, (0, 1), BOTH)
+                prepare(r + 1)
+                if r == TURN - 1:
+                    multiply(r, (2,), BOTH)
+                    if r < EARLY_THETA:
+                        multiply(r, (3,), (THETA,))
+                    prepare(r + 2)
+            else:
+                multiply(r, (0, 1), BOTH)
+            if r + AHEAD < N_ROUNDS:
+                load_round(r + AHEAD)
+            if r + AHEAD == N_ROUNDS:
                 load_rest()
             if r == N_ROUNDS - 1:
                 leave_psum(0, THETA)
@@ -372,10 +380,12 @@ def tile_attgcn_pa_k_kernel(
                 turn(0, THETA)
                 turn(0, PHI)
                 sum_over_time(0)
-            elif r >= LAG:
-                multiply(r - LAG, (2,), BOTH)
-            if r < EARLY_THETA:
-                multiply(r, (3,), (THETA,))
+            elif r != TURN - 1:
+                multiply(r, (2,), BOTH)
+                if r < EARLY_THETA:
+                    multiply(r, (3,), (THETA,))
+                if r >= TURN:
+                    prepare(r + 2)
 
         late = [(r, (2,), BOTH) for r in range(N_ROUNDS - 1 - LAG, N_ROUNDS)]
         late += [(r, (3,), (THETA,)) for r in range(EARLY_THETA, N_ROUNDS)] + [(r, (3,), (PHI,)) for r in range(N_ROUNDS)]

@@ -38,8 +38,10 @@ M_TILES = CHANNELS // P
 TURN = 1
 AHEAD = 3
 X_BEFORE = [[(0, 0, 1), (1, 0, 1)], [(0, 1, 1), (1, 1, 1), (0, 2, 1), (1, 2, 1)], [(0, 3, 1), (1, 3, 1)], [(0, 4, 1), (1, 4, 1)], [(0, 5, 1), (1, 5, 1)], [(0, 6, 1), (1, 6, 1)], [(0, 7, 1), (1, 7, 1)], []]
+EARLY_BOTH = 7
+EARLY_PHI = 0
 EARLY_THETA = 5
-BY_SCALAR = range(7)
+BY_SCALAR = ()
 
 FLOPS = 2 * BATCHES * TIMES * JOINTS * FEATURES * 2 * CHANNELS + 2 * BATCHES * JOINTS * JOINTS * CHANNELS * CHANNELS
 
@@ -66,9 +68,9 @@ def tile_attgcn_pa_k_kernel(
         keep = ctx.enter_context(tc.tile_pool(name="keep", bufs=1))
         x_pool = ctx.enter_context(tc.tile_pool(name="x_pool", bufs=2))
         regroup = ctx.enter_context(tc.tile_pool(name="regroup", bufs=2))
-        quant = ctx.enter_context(tc.tile_pool(name="quant", bufs=3))
+        quant = ctx.enter_context(tc.tile_pool(name="quant", bufs=max(3, 9 - EARLY_BOTH)))
         twice = ctx.enter_context(tc.tile_pool(name="twice", bufs=2))
-        results = ctx.enter_context(tc.tile_pool(name="results", bufs=6))
+        results = ctx.enter_context(tc.tile_pool(name="results", bufs=8))
         psum_acc = ctx.enter_context(tc.psum_pool(name="psum_acc", bufs=4))
         psum_work = ctx.enter_context(tc.psum_pool(name="psum_work", bufs=4))
 
@@ -243,7 +245,7 @@ def tile_attgcn_pa_k_kernel(
             y_of[s, w] = y
 
         def turn(b, w):
-            if w == PHI:
+            if w == PHI and b == 1:
                 means = psum_acc.tile([P, PACK, JOINTS], F32, tag="acc")
                 for j in range(PACK):
                     nc.tensor.matmul(means[:, j, :], lhsT=y_of[b, w][:, j, :], rhs=pick_joint[:], start=True, stop=True)
@@ -252,13 +254,18 @@ def tile_attgcn_pa_k_kernel(
             turned = psum_work.tile([P, PACK, P], F32, tag="work")
             for j in range(PACK):
                 nc.tensor.transpose(turned[:, j, :], y_of[b, w][:, j, :], ident[:])
-            turned_of[b] = turned
+            turned_of[b, w] = turned
 
-        def sum_over_time(b):
+        def sum_over_time(b, w):
             th = th_of[b]
+            if w == PHI:
+                th = keep.tile([P, JOINTS, PACK], F32, name="p_first")
+                p_of[b] = th[:].rearrange("p v j -> p j v")
             nc.vector.tensor_reduce(
-                out=th[:], in_=turned_of[b][:].rearrange("p j (t v) -> p v j t", t=T_HALF), axis=AXIS.X, op=ALU.add
+                out=th[:], in_=turned_of[b, w][:].rearrange("p j (t v) -> p v j t", t=T_HALF), axis=AXIS.X, op=ALU.add
             )
+            if w == PHI:
+                return
             nc.vector.tensor_tensor(
                 out=th[:], in0=th[:], in1=bias_sum[:].unsqueeze(1).to_broadcast([P, JOINTS, PACK]), op=ALU.add
             )
@@ -317,12 +324,12 @@ def tile_attgcn_pa_k_kernel(
                 out=a_plus[:, m, :], in0=a_bf[:, m, :], scalar1=lam_kappa_b[:, m : m + 1], scalar2=None, op0=ALU.add
             )
 
-        def finish(b, c, pair):
+        def finish(b, c, pair, by_scalar=False):
             cols = slice(CHUNK_COLS * c, CHUNK_COLS * (c + 1))
             g_ps = held["g", b, c, pair]
             result = results.tile([P, 2, CHUNK_COLS], F32)
             ms = slice(2 * pair, 2 * pair + 2)
-            if pair == 1 and b * N_CHUNKS + c in BY_SCALAR:
+            if by_scalar:
                 scaled = twice.tile([P, 2, CHUNK_COLS], F32)
                 nc.scalar.activation(out=scaled[:], in_=g_ps[:], func=ACT.Copy, scale=lam_col[:, 0:1])
                 nc.gpsimd.tensor_tensor(out=result[:], in0=scaled[:], in1=a_plus[:, ms, cols], op=ALU.add)
@@ -330,7 +337,14 @@ def tile_attgcn_pa_k_kernel(
                 nc.vector.scalar_tensor_tensor(
                     out=result[:], in0=g_ps[:], scalar=lam_col[:, 0:1], in1=a_plus[:, ms, cols], op0=ALU.mult, op1=ALU.add
                 )
-            nc.sync.dma_start(out=out_rows[b][:, ms, cols], in_=result[:])
+            held["r", b, c, pair] = result
+            if not by_scalar:
+                store(b, c, pair)
+
+        def store(b, c, pair):
+            cols = slice(CHUNK_COLS * c, CHUNK_COLS * (c + 1))
+            ms = slice(2 * pair, 2 * pair + 2)
+            nc.sync.dma_start(out=out_rows[b][:, ms, cols], in_=held["r", b, c, pair][:])
 
         def load_rest():
             for pair in range(M_TILES // 2):
@@ -365,6 +379,8 @@ def tile_attgcn_pa_k_kernel(
                     multiply(r, (2,), BOTH)
                     if r < EARLY_THETA:
                         multiply(r, (3,), (THETA,))
+                    if r < EARLY_PHI:
+                        multiply(r, (3,), (PHI,))
                     prepare(r + 2)
             else:
                 multiply(r, (0, 1), BOTH)
@@ -379,41 +395,82 @@ def tile_attgcn_pa_k_kernel(
                     add_bias_to_a(m)
                 turn(0, THETA)
                 turn(0, PHI)
-                sum_over_time(0)
+                sum_over_time(0, THETA)
+                sum_over_time(0, PHI)
             elif r != TURN - 1:
-                multiply(r, (2,), BOTH)
+                if r < EARLY_BOTH:
+                    multiply(r, (2,), BOTH)
                 if r < EARLY_THETA:
                     multiply(r, (3,), (THETA,))
+                if r < EARLY_PHI:
+                    multiply(r, (3,), (PHI,))
                 if r >= TURN:
                     prepare(r + 2)
 
-        late = [(r, (2,), BOTH) for r in range(N_ROUNDS - 1 - LAG, N_ROUNDS)]
-        late += [(r, (3,), (THETA,)) for r in range(EARLY_THETA, N_ROUNDS)] + [(r, (3,), (PHI,)) for r in range(N_ROUNDS)]
-        chunks = [(0, c) for c in range(N_CHUNKS)] + [None] * 0 + [(1, c) for c in range(N_CHUNKS)] + [None] * 3
-        done = 0
-        for s in range(len(chunks)):
-            now, before, third, fourth = [chunks[s - i] if s >= i else None for i in range(4)]
-            if third:
-                quantise_f(*third)
-                products(*third)
-            if fourth:
-                finish(*fourth, 0)
-                finish(*fourth, 1)
-            if now == (1, 0):
-                sum_over_time(1)
-            if now:
-                differences(*now)
-            if before:
-                tanh(*before)
-            if s == 1:
-                leave_psum(1, THETA)
-            if s == 3:
-                leave_psum(1, PHI)
-            upto = min(len(late), (4, 8, 12)[min(s, 2)])
-            for item in late[done:upto]:
-                multiply(*item)
-            done = upto
-            if s == 1:
-                turn(1, THETA)
-            if s == 3:
-                turn(1, PHI)
+        late = [(r, (2,), BOTH) for r in range(EARLY_BOTH, N_ROUNDS)]
+        late += [(r, (3,), (THETA,)) for r in range(EARLY_THETA, N_ROUNDS)] + [(r, (3,), (PHI,)) for r in range(EARLY_PHI, N_ROUNDS)]
+        def late_passes(n):
+            for _ in range(n):
+                multiply(*late.pop(0))
+
+        differences(0, 0)
+        differences(0, 1)
+        late_passes(2)
+        differences(0, 2)
+        tanh(0, 0)
+        late_passes(4)
+        quantise_f(0, 0)
+        tanh(0, 1)
+        leave_psum(1, THETA)
+        quantise_f(0, 1)
+        differences(0, 3)
+        late_passes(2)
+        tanh(0, 2)
+        products(0, 0)
+        tanh(0, 3)
+        finish(0, 0, 0)
+        quantise_f(0, 2)
+        late_passes(4)
+        leave_psum(1, PHI)
+        products(0, 1)
+        turn(1, THETA)
+        finish(0, 1, 0)
+        quantise_f(0, 3)
+        sum_over_time(1, THETA)
+        products(0, 2)
+        turn(1, PHI)
+        finish(0, 0, 1, by_scalar=True)
+        finish(0, 2, 1, by_scalar=True)
+        finish(0, 1, 1)
+        finish(0, 2, 0)
+        products(0, 3)
+        finish(0, 3, 1, by_scalar=True)
+        differences(1, 0)
+        store(0, 0, 1)
+        differences(1, 1)
+        differences(1, 2)
+        store(0, 2, 1)
+        tanh(1, 0)
+        quantise_f(1, 0)
+        finish(0, 3, 0, by_scalar=True)
+        differences(1, 3)
+        store(0, 3, 1)
+        tanh(1, 1)
+        quantise_f(1, 1)
+        store(0, 3, 0)
+        tanh(1, 2)
+        products(1, 0)
+        products(1, 1)
+        finish(1, 0, 0)
+        finish(1, 0, 1)
+        tanh(1, 3)
+        quantise_f(1, 2)
+        products(1, 2)
+        finish(1, 1, 0)
+        finish(1, 1, 1)
+        quantise_f(1, 3)
+        products(1, 3)
+        finish(1, 2, 0)
+        finish(1, 2, 1)
+        finish(1, 3, 0)
+        finish(1, 3, 1)

@@ -20,28 +20,30 @@ QUADRANTS = 4
 PLANES_PER_TILE = 4
 
 BATCHES, TIMES, JOINTS, FEATURES, CHANNELS = 2, 8, 32, 8192, 512
-T_HALF = TIMES // 2
-ROW_TILES = 2 * BATCHES
+T_SPLIT = 4
+TILES_PER_BATCH = TIMES // T_SPLIT
+ROW_TILES = BATCHES * TILES_PER_BATCH
 N_GROUPS = FEATURES // GROUP
 PHI, THETA = 0, 1
+BOTH = (THETA, PHI)
 
 ROUND_GROUPS = 2
 N_ROUNDS = N_GROUPS // ROUND_GROUPS
 ROUND_COLS = ROUND_GROUPS * GROUP
+ROUND_WORDS = ROUND_GROUPS * P
 BLOCKS = ROW_TILES * ROUND_GROUPS
-LAG = 0
+LOADS_AHEAD = 3
+assert 2 * N_GROUPS // PLANES_PER_TILE == N_ROUNDS
+
+EARLY_TILE_2 = 6
+EARLY_THETA_3 = 6
+EARLY_PHI_3 = 1
 
 U_CHUNK = 8
 N_CHUNKS = JOINTS // U_CHUNK
 CHUNK_COLS = U_CHUNK * JOINTS
 M_TILES = CHANNELS // P
-TURN = 1
-AHEAD = 3
-X_BEFORE = [[(0, 0, 1), (1, 0, 1)], [(0, 1, 1), (1, 1, 1), (0, 2, 1), (1, 2, 1)], [(0, 3, 1), (1, 3, 1)], [(0, 4, 1), (1, 4, 1)], [(0, 5, 1), (1, 5, 1)], [(0, 6, 1), (1, 6, 1)], [(0, 7, 1), (1, 7, 1)], []]
-EARLY_BOTH = 7
-EARLY_PHI = 0
-EARLY_THETA = 5
-BY_SCALAR = ()
+PAIR = 2
 
 FLOPS = 2 * BATCHES * TIMES * JOINTS * FEATURES * 2 * CHANNELS + 2 * BATCHES * JOINTS * JOINTS * CHANNELS * CHANNELS
 
@@ -68,15 +70,17 @@ def tile_attgcn_pa_k_kernel(
         keep = ctx.enter_context(tc.tile_pool(name="keep", bufs=1))
         x_pool = ctx.enter_context(tc.tile_pool(name="x_pool", bufs=2))
         regroup = ctx.enter_context(tc.tile_pool(name="regroup", bufs=2))
-        quant = ctx.enter_context(tc.tile_pool(name="quant", bufs=max(3, 9 - EARLY_BOTH)))
+        quant = ctx.enter_context(tc.tile_pool(name="quant", bufs=3))
+        d_pool = ctx.enter_context(tc.tile_pool(name="d_pool", bufs=3))
         twice = ctx.enter_context(tc.tile_pool(name="twice", bufs=2))
         results = ctx.enter_context(tc.tile_pool(name="results", bufs=8))
         psum_acc = ctx.enter_context(tc.psum_pool(name="psum_acc", bufs=4))
         psum_work = ctx.enter_context(tc.psum_pool(name="psum_work", bufs=4))
 
-        x_by_time = x.rearrange("b (rt t) v c -> (t v) (b rt) c", t=T_HALF)
+        x_rows = x.rearrange("b (rt t) v c -> (t v) (b rt) c", t=T_SPLIT)
         words_dram = [w.rearrange("g p n t -> p g (n t)").bitcast(I32) for w in (phi_w_words, theta_w_words)]
         scales_dram = [phi_w_scales, theta_w_scales]
+        a_rows = A.rearrange("(m p) u v -> p m (u v)", p=P)
         out_rows = [out[b].rearrange("(m p) u v -> p m (u v)", p=P) for b in range(BATCHES)]
 
         phi_words = keep.tile([P, N_GROUPS, CHANNELS], U32, align_bytes=64)
@@ -87,6 +91,8 @@ def tile_attgcn_pa_k_kernel(
         w_planes = [phi_planes, theta_planes]
         kappa_words = keep.tile([P, CHANNELS], U32, align_bytes=64)
         kappa_plane = keep.tile([P, CHANNELS], U8, align_bytes=64)
+        late_codes = keep.tile([P, N_ROUNDS, ROUND_WORDS], U32, align_bytes=64)
+        late_scales = keep.tile([P, N_ROUNDS, ROUND_WORDS], U8, align_bytes=64)
         a_bf = keep.tile([P, M_TILES, JOINTS * JOINTS], BF16)
         a_plus = keep.tile([P, M_TILES, JOINTS * JOINTS], F32)
         ident = keep.tile([P, P], F32)
@@ -110,33 +116,49 @@ def tile_attgcn_pa_k_kernel(
                     ].bitcast(I32),
                 )
 
-        def load_words(r):
+        def load_words(r, w):
             groups = slice(ROUND_GROUPS * r, ROUND_GROUPS * (r + 1))
-            for w in (THETA, PHI):
-                nc.sync.dma_start(out=w_words[w][:, groups, :].bitcast(I32), in_=words_dram[w][:, groups, :])
+            nc.sync.dma_start(out=w_words[w][:, groups, :].bitcast(I32), in_=words_dram[w][:, groups, :])
 
-        x_rounds = {}
+        x_of = {}
 
-        def load_x(b, first, n):
-            features = slice(ROUND_COLS * first, ROUND_COLS * (first + n))
-            x_chunk = x_pool.tile([P, 2, n * ROUND_COLS], BF16, tag="x%d%d" % (b, n))
-            nc.sync.dma_start(out=x_chunk[:], in_=x_by_time[:, 2 * b : 2 * b + 2, features])
-            for i in range(n):
-                x_rounds[b, first + i] = x_chunk[:, :, ROUND_COLS * i : ROUND_COLS * (i + 1)]
+        def load_x(b, r):
+            tiles = slice(TILES_PER_BATCH * b, TILES_PER_BATCH * (b + 1))
+            x_part = x_pool.tile([P, TILES_PER_BATCH, ROUND_COLS], BF16, tag="x%d" % b)
+            nc.sync.dma_start(out=x_part[:], in_=x_rows[:, tiles, ROUND_COLS * r : ROUND_COLS * (r + 1)])
+            x_of[b, r] = x_part
 
         def load_round(r):
-            for b, first, n in X_BEFORE[r]:
-                load_x(b, first, n)
             if r == 0:
-                load_scale_rows(0)
-                load_scale_rows(1)
-            elif r + 1 < N_ROUNDS:
+                for b in range(BATCHES):
+                    load_x(b, 0)
+                for w in BOTH:
+                    load_words(0, w)
+                    load_scale_rows(w)
+                return
+            for next_r in range(r + 1 if r > 1 else 1, min(r + 2, N_ROUNDS)):
+                for b in range(BATCHES):
+                    load_x(b, next_r)
+            if r + 1 < N_ROUNDS:
                 load_scale_rows(r + 1)
-            load_words(r)
+            for w in BOTH:
+                load_words(r, w)
+
+        def load_rest():
+            for m in range(0, M_TILES, PAIR):
+                nc.sync.dma_start(out=a_bf[:, m : m + PAIR, :], in_=a_rows[:, m : m + PAIR, :])
+            nc.sync.dma_start(
+                out=kappa_words[:].bitcast(I32), in_=kappa_w_words[0].rearrange("p n t -> p (n t)").bitcast(I32)
+            )
+            for quadrant in range(QUADRANTS):
+                nc.sync.dma_start(
+                    out=kappa_plane[32 * quadrant : 32 * quadrant + 4, :].bitcast(I32),
+                    in_=kappa_w_scales[0, 4 * quadrant : 4 * quadrant + 4, :].bitcast(I32),
+                )
 
         for plane in (phi_planes, theta_planes, kappa_plane):
             nc.vector.memset(plane[:].bitcast(I32), 0)
-        for r in range(AHEAD):
+        for r in range(LOADS_AHEAD):
             load_round(r)
 
         masks.make_identity(nc, ident[:])
@@ -153,132 +175,137 @@ def tile_attgcn_pa_k_kernel(
         nc.gpsimd.tensor_scalar(
             out=lam_kappa_b[:], in0=kappa_b_bf[:], scalar1=lam_col[:, 0:1], scalar2=0.0, op0=ALU.mult, op1=ALU.add
         )
-
         nc.vector.tensor_reduce(
-            out=pick_joint[:], in_=ident[:].rearrange("q (t v) -> q v t", t=T_HALF), axis=AXIS.X, op=ALU.add
+            out=pick_joint[:], in_=ident[:].rearrange("q (t v) -> q v t", t=T_SPLIT), axis=AXIS.X, op=ALU.add
         )
 
-        sorted_of, grouped_of, quantised = {}, {}, {}
+        sorted_of, grouped_of, packed_of, sums = {}, {}, {}, {}
 
         def sort_words(r):
             x_sorted = regroup.tile([P, BLOCKS, 2, P], F32)
-            half = BLOCKS // 2
+            half = BLOCKS // BATCHES
             for b in range(BATCHES):
                 nc.vector.tensor_copy(
-                    out=x_sorted[:, half * b : half * (b + 1)].rearrange("q (a g) h p -> q a g h p", a=2),
-                    in_=x_rounds[b, r].bitcast(F32).rearrange("q a (g p h) -> q a g h p", g=ROUND_GROUPS, h=2),
+                    out=x_sorted[:, half * b : half * (b + 1)].rearrange("q (a g) h p -> q a g h p", a=TILES_PER_BATCH),
+                    in_=x_of[b, r][:].bitcast(F32).rearrange("q a (g p h) -> q a g h p", g=ROUND_GROUPS, h=2),
                 )
             sorted_of[r] = x_sorted
 
         def transposes(r):
-            x_sorted = sorted_of[r]
             grouped = regroup.tile([P, BLOCKS, P * PACK], BF16, align_bytes=64)
             for k in range(0, BLOCKS, 2):
-                xt = psum_work.tile([P, 2, 2, P], F32, tag="work")
+                turned = psum_work.tile([P, 2, 2, P], F32, tag="work")
                 for i in range(2):
                     for h in range(2):
-                        nc.tensor.transpose(xt[:, i, h, :], x_sorted[:, k + i, h, :], ident[:])
+                        nc.tensor.transpose(turned[:, i, h, :], sorted_of[r][:, k + i, h, :], ident[:])
                 nc.scalar.copy(
                     out=grouped[:, k : k + 2, :].bitcast(F32).rearrange("p k (q h) -> p k q h", h=2),
-                    in_=xt[:].rearrange("p k h q -> p k q h"),
+                    in_=turned[:].rearrange("p k h q -> p k q h"),
                 )
             grouped_of[r] = grouped
 
-        late_codes = keep.tile([P, N_ROUNDS, ROUND_GROUPS * P], U32, align_bytes=64)
-        late_scales = keep.tile([P, N_ROUNDS, ROUND_GROUPS * P], U8, align_bytes=64)
-
         def quantise(r):
-            grouped = grouped_of[r]
-            codes = quant.tile([P, 3 * ROUND_GROUPS * P], U32, align_bytes=64)
-            scales = quant.tile([P, 3 * ROUND_GROUPS * P], U8, align_bytes=64)
-            n = ROUND_GROUPS
-            for a0, a1, out_codes, out_scales in (
-                (0, 2, codes[:, 0 : 2 * n * P], scales[:, 0 : 2 * n * P]),
-                (2, 3, codes[:, 2 * n * P : 3 * n * P], scales[:, 2 * n * P : 3 * n * P]),
-                (3, 4, late_codes[:, r, :], late_scales[:, r, :]),
-            ):
+            codes = quant.tile([P, 3 * ROUND_WORDS], U32, align_bytes=64)
+            scales = quant.tile([P, 3 * ROUND_WORDS], U8, align_bytes=64)
+            for a0, a1 in ((0, 2), (2, 3), (3, 4)):
+                if a0 < 3:
+                    words = slice(ROUND_WORDS * a0, ROUND_WORDS * a1)
+                    out_codes, out_scales = codes[:, words], scales[:, words]
+                else:
+                    out_codes, out_scales = late_codes[:, r, :], late_scales[:, r, :]
                 nc.vector.quantize_mx(
                     out=out_codes.bitcast(FP8X4),
                     scales=out_scales,
-                    in_=grouped[:, n * a0 : n * a1, :].rearrange("p k c -> p (k c)"),
+                    in_=grouped_of[r][:, ROUND_GROUPS * a0 : ROUND_GROUPS * a1, :].rearrange("p k c -> p (k c)"),
                 )
-            quantised[r] = (codes, scales)
+                for a in range(a0, a1):
+                    mine = slice(ROUND_WORDS * (a - a0), ROUND_WORDS * (a - a0 + 1))
+                    packed_of[a, r] = (out_codes[:, mine], out_scales[:, mine])
 
-        sums = {}
+        def prepare(r):
+            if r >= N_ROUNDS:
+                return
+            transposes(r)
+            if r == 0:
+                quantise(0)
+            if r + 1 < N_ROUNDS:
+                sort_words(r + 1)
+            if r > 0:
+                quantise(r)
 
         def multiply(r, tiles, weights):
             for w in weights:
                 for a in tiles:
-                    s, rt = divmod(a, 2)
+                    b, rt = divmod(a, TILES_PER_BATCH)
+                    codes, scales = packed_of[a, r]
                     for gi in range(ROUND_GROUPS):
                         g = ROUND_GROUPS * r + gi
-                        if a < 3:
-                            codes, scales = quantised[r]
-                            rows = slice(P * (a * ROUND_GROUPS + gi), P * (a * ROUND_GROUPS + gi + 1))
-                            lhs, lhs_scale = codes[:, rows], scales[:, rows]
-                        else:
-                            rows = slice(P * gi, P * (gi + 1))
-                            lhs, lhs_scale = late_codes[:, r, rows], late_scales[:, r, rows]
+                        rows = slice(P * gi, P * (gi + 1))
                         first = g == 0 and rt == 0
                         if first:
                             bank = psum_acc.tile([P, CHANNELS], F32, tag="acc")
-                            sums[s, w] = bank
-                        block, plane_start = g // PLANES_PER_TILE, 4 * (g % PLANES_PER_TILE)
+                            sums[b, w] = bank
+                        s, plane_start = g // PLANES_PER_TILE, 4 * (g % PLANES_PER_TILE)
                         nc.tensor.matmul_mx(
-                            out=sums[s, w][:],
-                            lhsT=lhs.bitcast(FP8X4),
-                            lhsT_scale=lhs_scale,
+                            out=sums[b, w][:],
+                            lhsT=codes[:, rows].bitcast(FP8X4),
+                            lhsT_scale=scales[:, rows],
                             rhs=w_words[w][:, g, :].bitcast(FP8X4),
-                            rhs_scale=w_planes[w][plane_start:P, block, :],
+                            rhs_scale=w_planes[w][plane_start:P, s, :],
                             start=first,
-                            stop=(g == N_GROUPS - 1 and rt == 1),
+                            stop=(g == N_GROUPS - 1 and rt == TILES_PER_BATCH - 1),
                         )
 
-        y_of, turned_of, p_of, th_of, held = {}, {}, {}, {}, {}
-        for b in range(BATCHES):
-            th_sums = keep.tile([P, JOINTS, PACK], F32, name="th%d" % b)
-            th_of[b] = th_sums
+        late = [(r, (2,), BOTH) for r in range(EARLY_TILE_2, N_ROUNDS)]
+        late += [(r, (3,), (THETA,)) for r in range(EARLY_THETA_3, N_ROUNDS)]
+        late += [(r, (3,), (PHI,)) for r in range(EARLY_PHI_3, N_ROUNDS)]
 
-        def leave_psum(s, w):
-            y = keep.tile([P, PACK, P], F32, name="y%d%d" % (s, w))
-            nc.scalar.copy(out=y[:], in_=sums[s, w][:].rearrange("q (p j) -> q j p", j=PACK))
-            y_of[s, w] = y
+        def late_passes(n):
+            for _ in range(n):
+                multiply(*late.pop(0))
+
+        y_of, turned_of, p_of, th_of, held = {}, {}, {}, {}, {}
+
+        def leave_psum(b, w):
+            y = keep.tile([P, PACK, P], F32, name="y%d%d" % (b, w))
+            nc.scalar.copy(out=y[:], in_=sums[b, w][:].rearrange("q (p j) -> q j p", j=PACK))
+            y_of[b, w] = y
 
         def turn(b, w):
-            if w == PHI and b == 1:
-                means = psum_acc.tile([P, PACK, JOINTS], F32, tag="acc")
-                for j in range(PACK):
-                    nc.tensor.matmul(means[:, j, :], lhsT=y_of[b, w][:, j, :], rhs=pick_joint[:], start=True, stop=True)
-                p_of[b] = means
-                return
             turned = psum_work.tile([P, PACK, P], F32, tag="work")
             for j in range(PACK):
                 nc.tensor.transpose(turned[:, j, :], y_of[b, w][:, j, :], ident[:])
             turned_of[b, w] = turned
 
         def sum_over_time(b, w):
-            th = th_of[b]
-            if w == PHI:
-                th = keep.tile([P, JOINTS, PACK], F32, name="p_first")
-                p_of[b] = th[:].rearrange("p v j -> p j v")
+            total = keep.tile([P, JOINTS, PACK], F32, name="total%d%d" % (b, w))
             nc.vector.tensor_reduce(
-                out=th[:], in_=turned_of[b, w][:].rearrange("p j (t v) -> p v j t", t=T_HALF), axis=AXIS.X, op=ALU.add
+                out=total[:],
+                in_=turned_of[b, w][:].rearrange("p j (t v) -> p v j t", t=T_SPLIT),
+                axis=AXIS.X,
+                op=ALU.add,
             )
             if w == PHI:
+                p_of[b] = total[:].rearrange("p v j -> p j v")
                 return
             nc.vector.tensor_tensor(
-                out=th[:], in0=th[:], in1=bias_sum[:].unsqueeze(1).to_broadcast([P, JOINTS, PACK]), op=ALU.add
+                out=total[:], in0=total[:], in1=bias_sum[:].unsqueeze(1).to_broadcast([P, JOINTS, PACK]), op=ALU.add
             )
+            th_of[b] = total
+
+        def phi_means_by_matmul(b):
+            means = psum_acc.tile([P, PACK, JOINTS], F32, tag="acc")
+            for j in range(PACK):
+                nc.tensor.matmul(means[:, j, :], lhsT=y_of[b, PHI][:, j, :], rhs=pick_joint[:], start=True, stop=True)
+            p_of[b] = means
 
         def differences(b, c):
             shape = [P, U_CHUNK, JOINTS, PACK]
-            d = twice.tile(shape, F32)
+            d = d_pool.tile(shape, F32)
+            p_part = p_of[b][:, :, U_CHUNK * c : U_CHUNK * (c + 1)].rearrange("p j u -> p u j")
             nc.vector.tensor_tensor(
                 out=d[:],
-                in0=p_of[b][:, :, U_CHUNK * c : U_CHUNK * (c + 1)]
-                .rearrange("p j u -> p u j")
-                .unsqueeze(2)
-                .to_broadcast(shape),
+                in0=p_part.unsqueeze(2).to_broadcast(shape),
                 in1=th_of[b][:].unsqueeze(1).to_broadcast(shape),
                 op=ALU.subtract,
             )
@@ -286,9 +313,8 @@ def tile_attgcn_pa_k_kernel(
 
         def tanh(b, c):
             f = twice.tile([P, CHUNK_COLS * PACK], BF16, align_bytes=64)
-            nc.scalar.activation(
-                out=f[:], in_=held["d", b, c][:].rearrange("p u v j -> p (u v j)"), func=ACT.Tanh, scale=1.0 / TIMES
-            )
+            d_flat = held["d", b, c][:].rearrange("p u v j -> p (u v j)")
+            nc.scalar.activation(out=f[:], in_=d_flat, func=ACT.Tanh, scale=1.0 / TIMES)
             held["f", b, c] = f
 
         def quantise_f(b, c):
@@ -299,14 +325,14 @@ def tile_attgcn_pa_k_kernel(
 
         def products(b, c):
             f_codes, f_scales = held["q", b, c]
-            for pair in range(M_TILES // 2):
-                g_ps = psum_work.tile([P, 2, CHUNK_COLS], F32, tag="work")
-                for i in range(2):
-                    channels = slice(P * (2 * pair + i), P * (2 * pair + i + 1))
+            for pair in range(M_TILES // PAIR):
+                g_ps = psum_work.tile([P, PAIR, CHUNK_COLS], F32, tag="work")
+                for i in range(PAIR):
+                    m = PAIR * pair + i
                     nc.tensor.matmul_mx(
                         out=g_ps[:, i, :],
-                        lhsT=kappa_words[:, channels].bitcast(FP8X4),
-                        lhsT_scale=kappa_plane[:, channels],
+                        lhsT=kappa_words[:, P * m : P * (m + 1)].bitcast(FP8X4),
+                        lhsT_scale=kappa_plane[:, P * m : P * (m + 1)],
                         rhs=f_codes[:].bitcast(FP8X4),
                         rhs_scale=f_scales[:],
                         start=True,
@@ -314,145 +340,106 @@ def tile_attgcn_pa_k_kernel(
                     )
                 held["g", b, c, pair] = g_ps
 
-        def add_bias_to_a(m):
-            if m >= 2:
-                nc.scalar.activation(
-                    out=a_plus[:, m, :], in_=a_bf[:, m, :], func=ACT.Identity, bias=lam_kappa_b[:, m : m + 1]
-                )
-                return
-            nc.vector.tensor_scalar(
-                out=a_plus[:, m, :], in0=a_bf[:, m, :], scalar1=lam_kappa_b[:, m : m + 1], scalar2=None, op0=ALU.add
-            )
-
-        def finish(b, c, pair, by_scalar=False):
-            cols = slice(CHUNK_COLS * c, CHUNK_COLS * (c + 1))
-            g_ps = held["g", b, c, pair]
-            result = results.tile([P, 2, CHUNK_COLS], F32)
-            ms = slice(2 * pair, 2 * pair + 2)
-            if by_scalar:
-                scaled = twice.tile([P, 2, CHUNK_COLS], F32)
-                nc.scalar.activation(out=scaled[:], in_=g_ps[:], func=ACT.Copy, scale=lam_col[:, 0:1])
-                nc.gpsimd.tensor_tensor(out=result[:], in0=scaled[:], in1=a_plus[:, ms, cols], op=ALU.add)
-            else:
-                nc.vector.scalar_tensor_tensor(
-                    out=result[:], in0=g_ps[:], scalar=lam_col[:, 0:1], in1=a_plus[:, ms, cols], op0=ALU.mult, op1=ALU.add
-                )
-            held["r", b, c, pair] = result
-            if not by_scalar:
-                store(b, c, pair)
-
         def store(b, c, pair):
-            cols = slice(CHUNK_COLS * c, CHUNK_COLS * (c + 1))
-            ms = slice(2 * pair, 2 * pair + 2)
+            ms, cols = slice(PAIR * pair, PAIR * (pair + 1)), slice(CHUNK_COLS * c, CHUNK_COLS * (c + 1))
             nc.sync.dma_start(out=out_rows[b][:, ms, cols], in_=held["r", b, c, pair][:])
 
-        def load_rest():
-            for pair in range(M_TILES // 2):
-                nc.sync.dma_start(
-                    out=a_bf[:, 2 * pair : 2 * pair + 2, :],
-                    in_=A.rearrange("(m p) u v -> p m (u v)", p=P)[:, 2 * pair : 2 * pair + 2, :],
-                )
-            nc.sync.dma_start(
-                out=kappa_words[:].bitcast(I32), in_=kappa_w_words[0].rearrange("p n t -> p (n t)").bitcast(I32)
+        def last_line(b, c, pair):
+            ms, cols = slice(PAIR * pair, PAIR * (pair + 1)), slice(CHUNK_COLS * c, CHUNK_COLS * (c + 1))
+            result = results.tile([P, PAIR, CHUNK_COLS], F32)
+            nc.vector.scalar_tensor_tensor(
+                out=result[:],
+                in0=held["g", b, c, pair][:],
+                scalar=lam_col[:, 0:1],
+                in1=a_plus[:, ms, cols],
+                op0=ALU.mult,
+                op1=ALU.add,
             )
-            for quadrant in range(QUADRANTS):
-                nc.sync.dma_start(
-                    out=kappa_plane[32 * quadrant : 32 * quadrant + 4, :].bitcast(I32),
-                    in_=kappa_w_scales[0, 4 * quadrant : 4 * quadrant + 4, :].bitcast(I32),
-                )
+            held["r", b, c, pair] = result
+            store(b, c, pair)
 
-        BOTH = (THETA, PHI)
-        def prepare(r):
-            if r < N_ROUNDS:
-                transposes(r)
-                quantise(r)
-            if r + 1 < N_ROUNDS:
-                sort_words(r + 1)
+        def last_line_shared(b, c, pair):
+            ms, cols = slice(PAIR * pair, PAIR * (pair + 1)), slice(CHUNK_COLS * c, CHUNK_COLS * (c + 1))
+            scaled = twice.tile([P, PAIR, CHUNK_COLS], F32)
+            result = results.tile([P, PAIR, CHUNK_COLS], F32)
+            nc.scalar.activation(out=scaled[:], in_=held["g", b, c, pair][:], func=ACT.Copy, scale=lam_col[:, 0:1])
+            nc.gpsimd.tensor_tensor(out=result[:], in0=scaled[:], in1=a_plus[:, ms, cols], op=ALU.add)
+            held["r", b, c, pair] = result
+
+        def add_kappa_b_to_a():
+            for m in range(M_TILES):
+                bias = lam_kappa_b[:, m : m + 1]
+                if m < M_TILES // 2:
+                    nc.vector.tensor_scalar(
+                        out=a_plus[:, m, :], in0=a_bf[:, m, :], scalar1=bias, scalar2=None, op0=ALU.add
+                    )
+                else:
+                    nc.scalar.activation(out=a_plus[:, m, :], in_=a_bf[:, m, :], func=ACT.Identity, bias=bias)
 
         sort_words(0)
         prepare(0)
         for r in range(N_ROUNDS):
-            if r < TURN:
-                multiply(r, (0, 1), BOTH)
-                prepare(r + 1)
-                if r == TURN - 1:
-                    multiply(r, (2,), BOTH)
-                    if r < EARLY_THETA:
-                        multiply(r, (3,), (THETA,))
-                    if r < EARLY_PHI:
-                        multiply(r, (3,), (PHI,))
-                    prepare(r + 2)
-            else:
-                multiply(r, (0, 1), BOTH)
-            if r + AHEAD < N_ROUNDS:
-                load_round(r + AHEAD)
-            if r + AHEAD == N_ROUNDS:
+            multiply(r, (0, 1), BOTH)
+            if r == 0:
+                prepare(1)
+            if r < EARLY_TILE_2:
+                multiply(r, (2,), BOTH)
+            if r < EARLY_THETA_3:
+                multiply(r, (3,), (THETA,))
+            if r < EARLY_PHI_3:
+                multiply(r, (3,), (PHI,))
+            prepare(r + 2)
+            if r + LOADS_AHEAD < N_ROUNDS:
+                load_round(r + LOADS_AHEAD)
+            elif r + LOADS_AHEAD == N_ROUNDS:
                 load_rest()
-            if r == N_ROUNDS - 1:
-                leave_psum(0, THETA)
-                leave_psum(0, PHI)
-                for m in range(M_TILES):
-                    add_bias_to_a(m)
-                turn(0, THETA)
-                turn(0, PHI)
-                sum_over_time(0, THETA)
-                sum_over_time(0, PHI)
-            elif r != TURN - 1:
-                if r < EARLY_BOTH:
-                    multiply(r, (2,), BOTH)
-                if r < EARLY_THETA:
-                    multiply(r, (3,), (THETA,))
-                if r < EARLY_PHI:
-                    multiply(r, (3,), (PHI,))
-                if r >= TURN:
-                    prepare(r + 2)
 
-        late = [(r, (2,), BOTH) for r in range(EARLY_BOTH, N_ROUNDS)]
-        late += [(r, (3,), (THETA,)) for r in range(EARLY_THETA, N_ROUNDS)] + [(r, (3,), (PHI,)) for r in range(EARLY_PHI, N_ROUNDS)]
-        def late_passes(n):
-            for _ in range(n):
-                multiply(*late.pop(0))
+        for w in BOTH:
+            leave_psum(0, w)
+        add_kappa_b_to_a()
+        for w in BOTH:
+            turn(0, w)
+        for w in BOTH:
+            sum_over_time(0, w)
 
-        differences(0, 0)
-        differences(0, 1)
-        late_passes(2)
-        differences(0, 2)
+        for c in range(3):
+            differences(0, c)
+        late_passes(6)
         tanh(0, 0)
-        late_passes(4)
-        quantise_f(0, 0)
         tanh(0, 1)
         leave_psum(1, THETA)
+        quantise_f(0, 0)
         quantise_f(0, 1)
         differences(0, 3)
-        late_passes(2)
+        late_passes(3)
         tanh(0, 2)
         products(0, 0)
         tanh(0, 3)
-        finish(0, 0, 0)
+        last_line(0, 0, 0)
         quantise_f(0, 2)
-        late_passes(4)
+        last_line(0, 0, 1)
+        late_passes(2)
         leave_psum(1, PHI)
         products(0, 1)
         turn(1, THETA)
-        finish(0, 1, 0)
+        last_line(0, 1, 0)
         quantise_f(0, 3)
         sum_over_time(1, THETA)
+        phi_means_by_matmul(1)
         products(0, 2)
-        turn(1, PHI)
-        finish(0, 0, 1, by_scalar=True)
-        finish(0, 2, 1, by_scalar=True)
-        finish(0, 1, 1)
-        finish(0, 2, 0)
+        last_line(0, 1, 1)
+        last_line_shared(0, 2, 1)
+        last_line(0, 2, 0)
         products(0, 3)
-        finish(0, 3, 1, by_scalar=True)
+        last_line_shared(0, 3, 1)
+
         differences(1, 0)
-        store(0, 0, 1)
+        store(0, 2, 1)
         differences(1, 1)
         differences(1, 2)
-        store(0, 2, 1)
         tanh(1, 0)
         quantise_f(1, 0)
-        finish(0, 3, 0, by_scalar=True)
+        last_line_shared(0, 3, 0)
         differences(1, 3)
         store(0, 3, 1)
         tanh(1, 1)
@@ -461,16 +448,14 @@ def tile_attgcn_pa_k_kernel(
         tanh(1, 2)
         products(1, 0)
         products(1, 1)
-        finish(1, 0, 0)
-        finish(1, 0, 1)
-        tanh(1, 3)
-        quantise_f(1, 2)
-        products(1, 2)
-        finish(1, 1, 0)
-        finish(1, 1, 1)
-        quantise_f(1, 3)
-        products(1, 3)
-        finish(1, 2, 0)
-        finish(1, 2, 1)
-        finish(1, 3, 0)
-        finish(1, 3, 1)
+        for c in range(N_CHUNKS):
+            if c == 1:
+                products(1, 2)
+            if c == 2:
+                products(1, 3)
+            for pair in range(M_TILES // PAIR):
+                last_line(1, c, pair)
+            if c == 0:
+                tanh(1, 3)
+            if c < 2:
+                quantise_f(1, c + 2)

from contextlib import ExitStack

import concourse.masks as masks
import concourse.mybir as mybir

F32 = mybir.dt.float32
BF16 = mybir.dt.bfloat16
I32 = mybir.dt.int32
U32 = mybir.dt.uint32
U8 = mybir.dt.uint8
FP8X4 = mybir.dt.float8_e4m3fn_x4
ALU = mybir.AluOpType
ACT = mybir.ActivationFunctionType
AXIS = mybir.AxisListType

P = 128
PACK = 4
GROUP = P * PACK
QUADRANTS = 4
PLANES_PER_TILE = 4

BATCHES, TIMES, JOINTS, FEATURES, CHANNELS = 2, 8, 32, 8192, 512
T_SPLIT = 4
TILES_PER_BATCH = TIMES // T_SPLIT
ROW_TILES = BATCHES * TILES_PER_BATCH
N_GROUPS = FEATURES // GROUP
PHI, THETA = 0, 1
BOTH = (THETA, PHI)

ROUND_GROUPS = 2
N_ROUNDS = N_GROUPS // ROUND_GROUPS
ROUND_COLS = ROUND_GROUPS * GROUP
ROUND_WORDS = ROUND_GROUPS * P
BLOCKS = ROW_TILES * ROUND_GROUPS
LOADS_AHEAD = 3
assert 2 * N_GROUPS // PLANES_PER_TILE == N_ROUNDS

EARLY_TILE_2 = 6
EARLY_THETA_3 = 6
EARLY_PHI_3 = 1

U_CHUNK = 8
N_CHUNKS = JOINTS // U_CHUNK
CHUNK_COLS = U_CHUNK * JOINTS
M_TILES = CHANNELS // P
PAIR = 2

FLOPS = 2 * BATCHES * TIMES * JOINTS * FEATURES * 2 * CHANNELS + 2 * BATCHES * JOINTS * JOINTS * CHANNELS * CHANNELS


def tile_attgcn_pa_k_kernel(
    tc,
    x,
    A,
    lam,
    phi_w_words,
    phi_w_scales,
    phi_b,
    theta_w_words,
    theta_w_scales,
    theta_b,
    kappa_w_words,
    kappa_w_scales,
    kappa_b,
    out,
):
    nc = tc.nc
    with ExitStack() as ctx:
        ctx.enter_context(tc.manual_schedule())
        keep = ctx.enter_context(tc.tile_pool(name="keep", bufs=1))
        x_pool = ctx.enter_context(tc.tile_pool(name="x_pool", bufs=2))
        regroup = ctx.enter_context(tc.tile_pool(name="regroup", bufs=2))
        quant = ctx.enter_context(tc.tile_pool(name="quant", bufs=3))
        d_pool = ctx.enter_context(tc.tile_pool(name="d_pool", bufs=3))
        twice = ctx.enter_context(tc.tile_pool(name="twice", bufs=2))
        results = ctx.enter_context(tc.tile_pool(name="results", bufs=8))
        psum_acc = ctx.enter_context(tc.psum_pool(name="psum_acc", bufs=4))
        psum_work = ctx.enter_context(tc.psum_pool(name="psum_work", bufs=4))

        x_rows = x.rearrange("b (rt t) v c -> (t v) (b rt) c", t=T_SPLIT)
        words_dram = [w.rearrange("g p n t -> p g (n t)").bitcast(I32) for w in (phi_w_words, theta_w_words)]
        scales_dram = [phi_w_scales, theta_w_scales]
        a_rows = A.rearrange("(m p) u v -> p m (u v)", p=P)
        out_rows = [out[b].rearrange("(m p) u v -> p m (u v)", p=P) for b in range(BATCHES)]

        phi_words = keep.tile([P, N_GROUPS, CHANNELS], U32, align_bytes=64)
        theta_words = keep.tile([P, N_GROUPS, CHANNELS], U32, align_bytes=64)
        w_words = [phi_words, theta_words]
        phi_planes = keep.tile([P, N_GROUPS // PLANES_PER_TILE, CHANNELS], U8, align_bytes=64)
        theta_planes = keep.tile([P, N_GROUPS // PLANES_PER_TILE, CHANNELS], U8, align_bytes=64)
        w_planes = [phi_planes, theta_planes]
        kappa_words = keep.tile([P, CHANNELS], U32, align_bytes=64)
        kappa_plane = keep.tile([P, CHANNELS], U8, align_bytes=64)
        late_codes = keep.tile([P, N_ROUNDS, ROUND_WORDS], U32, align_bytes=64)
        late_scales = keep.tile([P, N_ROUNDS, ROUND_WORDS], U8, align_bytes=64)
        a_bf = keep.tile([P, M_TILES, JOINTS * JOINTS], BF16)
        a_plus = keep.tile([P, M_TILES, JOINTS * JOINTS], F32)
        ident = keep.tile([P, P], F32)
        pick_joint = keep.tile([P, JOINTS], F32)
        lam_bf = keep.tile([P, 1], BF16)
        lam_col = keep.tile([P, 1], F32)
        kappa_b_bf = keep.tile([P, M_TILES], BF16)
        lam_kappa_b = keep.tile([P, M_TILES], F32)
        phi_b_bf = keep.tile([P, PACK], BF16)
        theta_b_bf = keep.tile([P, PACK], BF16)
        bias_diff = keep.tile([P, PACK], F32)
        bias_sum = keep.tile([P, PACK], F32)

        def load_scale_rows(k):
            w, s = k % 2, k // 2
            for quadrant in range(QUADRANTS):
                nc.sync.dma_start(
                    out=w_planes[w][32 * quadrant : 32 * quadrant + 16, s, :].bitcast(I32),
                    in_=scales_dram[w][
                        PLANES_PER_TILE * s : PLANES_PER_TILE * (s + 1), 4 * quadrant : 4 * quadrant + 4, :
                    ].bitcast(I32),
                )

        def load_words(r, w):
            groups = slice(ROUND_GROUPS * r, ROUND_GROUPS * (r + 1))
            nc.sync.dma_start(out=w_words[w][:, groups, :].bitcast(I32), in_=words_dram[w][:, groups, :])

        x_of = {}

        def load_x(b, r):
            tiles = slice(TILES_PER_BATCH * b, TILES_PER_BATCH * (b + 1))
            x_part = x_pool.tile([P, TILES_PER_BATCH, ROUND_COLS], BF16, tag="x%d" % b)
            nc.sync.dma_start(out=x_part[:], in_=x_rows[:, tiles, ROUND_COLS * r : ROUND_COLS * (r + 1)])
            x_of[b, r] = x_part

        def load_round(r):
            if r == 0:
                for b in range(BATCHES):
                    load_x(b, 0)
                for w in BOTH:
                    load_words(0, w)
                    load_scale_rows(w)
                return
            for next_r in range(r + 1 if r > 1 else 1, min(r + 2, N_ROUNDS)):
                for b in range(BATCHES):
                    load_x(b, next_r)
            if r + 1 < N_ROUNDS:
                load_scale_rows(r + 1)
            for w in BOTH:
                load_words(r, w)

        def load_rest():
            for m in range(0, M_TILES, PAIR):
                nc.sync.dma_start(out=a_bf[:, m : m + PAIR, :], in_=a_rows[:, m : m + PAIR, :])
            nc.sync.dma_start(
                out=kappa_words[:].bitcast(I32), in_=kappa_w_words[0].rearrange("p n t -> p (n t)").bitcast(I32)
            )
            for quadrant in range(QUADRANTS):
                nc.sync.dma_start(
                    out=kappa_plane[32 * quadrant : 32 * quadrant + 4, :].bitcast(I32),
                    in_=kappa_w_scales[0, 4 * quadrant : 4 * quadrant + 4, :].bitcast(I32),
                )

        for plane in (phi_planes, theta_planes, kappa_plane):
            nc.vector.memset(plane[:].bitcast(I32), 0)
        for r in range(LOADS_AHEAD):
            load_round(r)

        masks.make_identity(nc, ident[:])
        nc.gpsimd.dma_start(out=lam_bf[:], in_=lam.partition_broadcast(P))
        nc.gpsimd.dma_start(out=phi_b_bf[:], in_=phi_b.rearrange("(p j) -> p j", j=PACK))
        nc.gpsimd.dma_start(out=theta_b_bf[:], in_=theta_b.rearrange("(p j) -> p j", j=PACK))
        with nc.allow_non_contiguous_dma(reason="512 bias values, one output channel to a partition"):
            nc.gpsimd.dma_start(out=kappa_b_bf[:], in_=kappa_b.rearrange("(m p) -> p m", p=P))
        nc.gpsimd.tensor_copy(out=lam_col[:], in_=lam_bf[:])
        nc.gpsimd.tensor_tensor(out=bias_diff[:], in0=theta_b_bf[:], in1=phi_b_bf[:], op=ALU.subtract)
        nc.gpsimd.tensor_scalar(
            out=bias_sum[:], in0=bias_diff[:], scalar1=float(TIMES), scalar2=0.0, op0=ALU.mult, op1=ALU.add
        )
        nc.gpsimd.tensor_scalar(
            out=lam_kappa_b[:], in0=kappa_b_bf[:], scalar1=lam_col[:, 0:1], scalar2=0.0, op0=ALU.mult, op1=ALU.add
        )
        nc.vector.tensor_reduce(
            out=pick_joint[:], in_=ident[:].rearrange("q (t v) -> q v t", t=T_SPLIT), axis=AXIS.X, op=ALU.add
        )

        sorted_of, grouped_of, packed_of, sums = {}, {}, {}, {}

        def sort_words(r):
            x_sorted = regroup.tile([P, BLOCKS, 2, P], F32)
            half = BLOCKS // BATCHES
            for b in range(BATCHES):
                nc.vector.tensor_copy(
                    out=x_sorted[:, half * b : half * (b + 1)].rearrange("q (a g) h p -> q a g h p", a=TILES_PER_BATCH),
                    in_=x_of[b, r][:].bitcast(F32).rearrange("q a (g p h) -> q a g h p", g=ROUND_GROUPS, h=2),
                )
            sorted_of[r] = x_sorted

        def transposes(r):
            grouped = regroup.tile([P, BLOCKS, P * PACK], BF16, align_bytes=64)
            for k in range(0, BLOCKS, 2):
                turned = psum_work.tile([P, 2, 2, P], F32, tag="work")
                for i in range(2):
                    for h in range(2):
                        nc.tensor.transpose(turned[:, i, h, :], sorted_of[r][:, k + i, h, :], ident[:])
                nc.scalar.copy(
                    out=grouped[:, k : k + 2, :].bitcast(F32).rearrange("p k (q h) -> p k q h", h=2),
                    in_=turned[:].rearrange("p k h q -> p k q h"),
                )
            grouped_of[r] = grouped

        def quantise(r):
            codes = quant.tile([P, 3 * ROUND_WORDS], U32, align_bytes=64)
            scales = quant.tile([P, 3 * ROUND_WORDS], U8, align_bytes=64)
            for a0, a1 in ((0, 2), (2, 3), (3, 4)):
                if a0 < 3:
                    words = slice(ROUND_WORDS * a0, ROUND_WORDS * a1)
                    out_codes, out_scales = codes[:, words], scales[:, words]
                else:
                    out_codes, out_scales = late_codes[:, r, :], late_scales[:, r, :]
                nc.vector.quantize_mx(
                    out=out_codes.bitcast(FP8X4),
                    scales=out_scales,
                    in_=grouped_of[r][:, ROUND_GROUPS * a0 : ROUND_GROUPS * a1, :].rearrange("p k c -> p (k c)"),
                )
                for a in range(a0, a1):
                    mine = slice(ROUND_WORDS * (a - a0), ROUND_WORDS * (a - a0 + 1))
                    packed_of[a, r] = (out_codes[:, mine], out_scales[:, mine])

        def prepare(r):
            if r >= N_ROUNDS:
                return
            transposes(r)
            if r == 0:
                quantise(0)
            if r + 1 < N_ROUNDS:
                sort_words(r + 1)
            if r > 0:
                quantise(r)

        def multiply(r, tiles, weights):
            for w in weights:
                for a in tiles:
                    b, rt = divmod(a, TILES_PER_BATCH)
                    codes, scales = packed_of[a, r]
                    for gi in range(ROUND_GROUPS):
                        g = ROUND_GROUPS * r + gi
                        rows = slice(P * gi, P * (gi + 1))
                        first = g == 0 and rt == 0
                        if first:
                            bank = psum_acc.tile([P, CHANNELS], F32, tag="acc")
                            sums[b, w] = bank
                        s, plane_start = g // PLANES_PER_TILE, 4 * (g % PLANES_PER_TILE)
                        nc.tensor.matmul_mx(
                            out=sums[b, w][:],
                            lhsT=codes[:, rows].bitcast(FP8X4),
                            lhsT_scale=scales[:, rows],
                            rhs=w_words[w][:, g, :].bitcast(FP8X4),
                            rhs_scale=w_planes[w][plane_start:P, s, :],
                            start=first,
                            stop=(g == N_GROUPS - 1 and rt == TILES_PER_BATCH - 1),
                        )

        late = [(r, (2,), BOTH) for r in range(EARLY_TILE_2, N_ROUNDS)]
        late += [(r, (3,), (THETA,)) for r in range(EARLY_THETA_3, N_ROUNDS)]
        late += [(r, (3,), (PHI,)) for r in range(EARLY_PHI_3, N_ROUNDS)]

        def late_passes(n):
            for _ in range(n):
                multiply(*late.pop(0))

        y_of, turned_of, p_of, th_of, held = {}, {}, {}, {}, {}

        def leave_psum(b, w):
            y = keep.tile([P, PACK, P], F32, name="y%d%d" % (b, w))
            nc.scalar.copy(out=y[:], in_=sums[b, w][:].rearrange("q (p j) -> q j p", j=PACK))
            y_of[b, w] = y

        def turn(b, w):
            turned = psum_work.tile([P, PACK, P], F32, tag="work")
            for j in range(PACK):
                nc.tensor.transpose(turned[:, j, :], y_of[b, w][:, j, :], ident[:])
            turned_of[b, w] = turned

        def sum_over_time(b, w):
            total = keep.tile([P, JOINTS, PACK], F32, name="total%d%d" % (b, w))
            nc.vector.tensor_reduce(
                out=total[:],
                in_=turned_of[b, w][:].rearrange("p j (t v) -> p v j t", t=T_SPLIT),
                axis=AXIS.X,
                op=ALU.add,
            )
            if w == PHI:
                p_of[b] = total[:].rearrange("p v j -> p j v")
                return
            nc.vector.tensor_tensor(
                out=total[:], in0=total[:], in1=bias_sum[:].unsqueeze(1).to_broadcast([P, JOINTS, PACK]), op=ALU.add
            )
            th_of[b] = total

        def phi_means_by_matmul(b):
            means = psum_acc.tile([P, PACK, JOINTS], F32, tag="acc")
            for j in range(PACK):
                nc.tensor.matmul(means[:, j, :], lhsT=y_of[b, PHI][:, j, :], rhs=pick_joint[:], start=True, stop=True)
            p_of[b] = means

        def differences(b, c):
            shape = [P, U_CHUNK, JOINTS, PACK]
            d = d_pool.tile(shape, F32)
            p_part = p_of[b][:, :, U_CHUNK * c : U_CHUNK * (c + 1)].rearrange("p j u -> p u j")
            nc.vector.tensor_tensor(
                out=d[:],
                in0=p_part.unsqueeze(2).to_broadcast(shape),
                in1=th_of[b][:].unsqueeze(1).to_broadcast(shape),
                op=ALU.subtract,
            )
            held["d", b, c] = d

        def tanh(b, c):
            f = twice.tile([P, CHUNK_COLS * PACK], BF16, align_bytes=64)
            d_flat = held["d", b, c][:].rearrange("p u v j -> p (u v j)")
            nc.scalar.activation(out=f[:], in_=d_flat, func=ACT.Tanh, scale=1.0 / TIMES)
            held["f", b, c] = f

        def quantise_f(b, c):
            f_codes = twice.tile([P, CHUNK_COLS], U32, align_bytes=64)
            f_scales = twice.tile([P, CHUNK_COLS], U8, align_bytes=64)
            nc.vector.quantize_mx(out=f_codes[:].bitcast(FP8X4), scales=f_scales[:], in_=held["f", b, c][:])
            held["q", b, c] = (f_codes, f_scales)

        def products(b, c):
            f_codes, f_scales = held["q", b, c]
            for pair in range(M_TILES // PAIR):
                g_ps = psum_work.tile([P, PAIR, CHUNK_COLS], F32, tag="work")
                for i in range(PAIR):
                    m = PAIR * pair + i
                    nc.tensor.matmul_mx(
                        out=g_ps[:, i, :],
                        lhsT=kappa_words[:, P * m : P * (m + 1)].bitcast(FP8X4),
                        lhsT_scale=kappa_plane[:, P * m : P * (m + 1)],
                        rhs=f_codes[:].bitcast(FP8X4),
                        rhs_scale=f_scales[:],
                        start=True,
                        stop=True,
                    )
                held["g", b, c, pair] = g_ps

        def store(b, c, pair):
            ms, cols = slice(PAIR * pair, PAIR * (pair + 1)), slice(CHUNK_COLS * c, CHUNK_COLS * (c + 1))
            nc.sync.dma_start(out=out_rows[b][:, ms, cols], in_=held["r", b, c, pair][:])

        def last_line(b, c, pair):
            ms, cols = slice(PAIR * pair, PAIR * (pair + 1)), slice(CHUNK_COLS * c, CHUNK_COLS * (c + 1))
            result = results.tile([P, PAIR, CHUNK_COLS], F32)
            nc.vector.scalar_tensor_tensor(
                out=result[:],
                in0=held["g", b, c, pair][:],
                scalar=lam_col[:, 0:1],
                in1=a_plus[:, ms, cols],
                op0=ALU.mult,
                op1=ALU.add,
            )
            held["r", b, c, pair] = result
            store(b, c, pair)

        def last_line_shared(b, c, pair):
            ms, cols = slice(PAIR * pair, PAIR * (pair + 1)), slice(CHUNK_COLS * c, CHUNK_COLS * (c + 1))
            scaled = twice.tile([P, PAIR, CHUNK_COLS], F32)
            result = results.tile([P, PAIR, CHUNK_COLS], F32)
            nc.scalar.activation(out=scaled[:], in_=held["g", b, c, pair][:], func=ACT.Copy, scale=lam_col[:, 0:1])
            nc.gpsimd.tensor_tensor(out=result[:], in0=scaled[:], in1=a_plus[:, ms, cols], op=ALU.add)
            held["r", b, c, pair] = result

        def add_kappa_b_to_a():
            for m in range(M_TILES):
                bias = lam_kappa_b[:, m : m + 1]
                if m < M_TILES // 2:
                    nc.vector.tensor_scalar(
                        out=a_plus[:, m, :], in0=a_bf[:, m, :], scalar1=bias, scalar2=None, op0=ALU.add
                    )
                else:
                    nc.scalar.activation(out=a_plus[:, m, :], in_=a_bf[:, m, :], func=ACT.Identity, bias=bias)

        sort_words(0)
        prepare(0)
        for r in range(N_ROUNDS):
            multiply(r, (0, 1), BOTH)
            if r == 0:
                prepare(1)
            if r < EARLY_TILE_2:
                multiply(r, (2,), BOTH)
            if r < EARLY_THETA_3:
                multiply(r, (3,), (THETA,))
            if r < EARLY_PHI_3:
                multiply(r, (3,), (PHI,))
            prepare(r + 2)
            if r + LOADS_AHEAD < N_ROUNDS:
                load_round(r + LOADS_AHEAD)
            elif r + LOADS_AHEAD == N_ROUNDS:
                load_rest()

        for w in BOTH:
            leave_psum(0, w)
        add_kappa_b_to_a()
        for w in BOTH:
            turn(0, w)
        for w in BOTH:
            sum_over_time(0, w)

        for c in range(3):
            differences(0, c)
        late_passes(6)
        tanh(0, 0)
        tanh(0, 1)
        leave_psum(1, THETA)
        quantise_f(0, 0)
        quantise_f(0, 1)
        differences(0, 3)
        late_passes(3)
        tanh(0, 2)
        products(0, 0)
        tanh(0, 3)
        last_line(0, 0, 0)
        quantise_f(0, 2)
        last_line(0, 0, 1)
        late_passes(2)
        leave_psum(1, PHI)
        products(0, 1)
        turn(1, THETA)
        last_line(0, 1, 0)
        quantise_f(0, 3)
        sum_over_time(1, THETA)
        phi_means_by_matmul(1)
        products(0, 2)
        last_line(0, 1, 1)
        last_line_shared(0, 2, 1)
        last_line(0, 2, 0)
        products(0, 3)
        last_line_shared(0, 3, 1)

        differences(1, 0)
        store(0, 2, 1)
        differences(1, 1)
        differences(1, 2)
        tanh(1, 0)
        quantise_f(1, 0)
        last_line_shared(0, 3, 0)
        differences(1, 3)
        store(0, 3, 1)
        tanh(1, 1)
        quantise_f(1, 1)
        store(0, 3, 0)
        tanh(1, 2)
        products(1, 0)
        products(1, 1)
        for c in range(N_CHUNKS):
            if c == 1:
                products(1, 2)
            if c == 2:
                products(1, 3)
            for pair in range(M_TILES // PAIR):
                last_line(1, c, pair)
            if c == 0:
                tanh(1, 3)
            if c < 2:
                quantise_f(1, c + 2)
